import numpy as np
import ml_dtypes


def mxq(x, axis, fmt="e4m3"):
    dtype, down = {"e4m3": (ml_dtypes.float8_e4m3fn, 7), "e5m2": (ml_dtypes.float8_e5m2, 14)}[fmt]
    v = np.moveaxis(np.asarray(x, np.float32).astype(ml_dtypes.bfloat16).astype(np.float64), axis, -1)
    blocks = v.reshape(v.shape[:-1] + (-1, 32))
    amax = np.abs(blocks).max(-1, keepdims=True)
    byte = np.maximum(np.where(amax > 0, np.frexp(amax)[1] - 1 + 127, 0) - down, 1)
    scale = np.exp2(byte - 127.0)
    codes = (blocks / scale).astype(np.float32).astype(dtype).astype(np.float64)
    return np.moveaxis((codes * scale).reshape(v.shape), -1, axis)


WIDE = False


def mx_kscale(k):
    if not WIDE:
        return np.ones(k)
    levels = np.array([10, -10, 5, -5, 0])
    a = np.random.permutation(np.resize(levels, k // 512 * 4)).reshape(k // 512, 4)
    idx = np.arange(k)
    return np.exp2(a[idx // 512, idx % 128 // 32])


BF16 = ml_dtypes.bfloat16


def bf(x):
    return np.asarray(x, np.float32).astype(BF16)


def f64(x):
    return np.asarray(x).astype(np.float64)


B, C_IN, H, W, C_OUT, K, PAD, STRIDE = 128, 512, 5, 5, 128, 4, 1, 1
OUT_H = (H + 2 * PAD - K) // STRIDE + 1
OUT_W = (W + 2 * PAD - K) // STRIDE + 1
L = OUT_H * OUT_W
IN_FEAT = C_IN * K * K
BLK = 32
G = BLK // int(np.gcd(BLK, K * K))


def setup_inputs():
    sc = np.repeat(mx_kscale(IN_FEAT)[::BLK][:C_IN // G], G)
    sf = np.repeat(sc, K * K)
    return {"x": bf(np.random.standard_normal((B, C_IN, H, W)) * sc[None, :, None, None]),
            "weight": bf(np.random.standard_normal((L, IN_FEAT, C_OUT)) / np.sqrt(IN_FEAT) / sf[None, :, None]),
            "bias": bf(np.random.standard_normal((L, C_OUT)) * 0.3)}


def _unfold(x):
    xp = np.pad(x, ((0, 0), (0, 0), (PAD, PAD), (PAD, PAD)))
    cols = []
    for i in range(K):
        for j in range(K):
            cols.append(xp[:, :, i:i + OUT_H * STRIDE:STRIDE, j:j + OUT_W * STRIDE:STRIDE])
    p = np.stack(cols, axis=2)
    p = p.reshape(x.shape[0], C_IN * K * K, L)
    return np.ascontiguousarray(p.transpose(0, 2, 1))


def reference(x, weight, bias):
    x = f64(x)
    patches = _unfold(x)
    pq = mxq(patches, 2, "e4m3")
    wq = mxq(f64(weight), 1, "e4m3")
    out = (pq.transpose(1, 0, 2) @ wq).transpose(1, 0, 2)
    out = out + f64(bias)[None]
    out = out.transpose(0, 2, 1).reshape(x.shape[0], C_OUT, OUT_H, OUT_W)
    out = np.maximum(out, 0.0)
    Bn = out.shape[0]
    out = out.reshape(Bn, C_OUT, OUT_H // 2, 2, OUT_W // 2, 2).max(axis=(3, 5))
    return out

@@ -1,0 +1,210 @@
+from contextlib import ExitStack
+
+import concourse.masks as masks
+import concourse.mybir as mybir
+
+BF16 = mybir.dt.bfloat16
+F32 = mybir.dt.float32
+U32 = mybir.dt.uint32
+U8 = mybir.dt.uint8
+FP8X4 = mybir.dt.float8_e4m3fn_x4
+MAX = mybir.AluOpType.max
+ADD = mybir.AluOpType.add
+
+P = 128
+PACK = 4
+BATCH = 128
+C_OUT = 128
+IMG = 5
+PADDED = IMG + 2
+KER = 4
+OUT_HW = 4
+CLASSES = 4
+PASSES = CLASSES * KER
+HALF = PASSES // 2
+PIXELS = IMG * IMG
+X_CHUNKS = 4
+V_CHUNK = 64 // X_CHUNKS
+RAW_BUFS = 3
+
+FLOPS = 2 * BATCH * (512 * KER * KER) * C_OUT * OUT_HW * OUT_HW
+
+
+def regroup(copy, grouped, rows):
+    copy(out=grouped, in_=rows.rearrange("p u t c -> p u c t"))
+
+
+def tile_normalizedlocalmapping_k_kernel(tc, x, weight, bias, out):
+    nc = tc.nc
+    positions = [(oh, ow) for ow in range(OUT_HW) for oh in range(OUT_HW)]
+
+    with ExitStack() as ctx:
+        const = ctx.enter_context(tc.tile_pool(name="const", bufs=1))
+        raw_pool = ctx.enter_context(tc.tile_pool(name="raw", bufs=RAW_BUFS))
+        grouped_pool = ctx.enter_context(tc.tile_pool(name="grouped", bufs=2))
+        codes_pool = ctx.enter_context(tc.tile_pool(name="codes", bufs=2))
+        work = ctx.enter_context(tc.tile_pool(name="work", bufs=2))
+        acc_pool = ctx.enter_context(tc.psum_pool(name="acc", bufs=1))
+
+        raw = {}
+        grouped = {}
+        quantised = {}
+
+        def load_weights(n):
+            oh, ow = positions[n]
+            rows = weight[oh * OUT_HW + ow].rearrange(
+                "(v s e k) o -> e v s (k o)", s=CLASSES, e=2, k=KER * KER
+            )
+            raw[n] = raw_pool.tile([P, PASSES, PACK, C_OUT], BF16, name="raw")
+            for e in range(2):
+                nc.sync.dma_start(
+                    out=raw[n][e:P:2].rearrange("p (s i) t o -> p s (i t o)", s=CLASSES),
+                    in_=rows[e],
+                )
+
+        def regroup_weights(n):
+            by_vector = grouped_pool.tile([P, HALF, C_OUT, PACK], BF16, name="by_vector", align_bytes=64)
+            by_scalar = grouped_pool.tile([P, HALF, C_OUT, PACK], BF16, name="by_scalar", align_bytes=64)
+            regroup(nc.vector.tensor_copy, by_vector[:], raw[n][:, 0:HALF])
+            regroup(nc.scalar.copy, by_scalar[:], raw[n][:, HALF:PASSES])
+            grouped[n] = (by_vector, by_scalar)
+            if n + RAW_BUFS < len(positions):
+                load_weights(n + RAW_BUFS)
+
+        def quantise_weights(n):
+            w_codes = codes_pool.tile([P, PASSES, C_OUT], U32, name="w_codes", align_bytes=64)
+            w_scales = codes_pool.tile([P, PASSES, C_OUT], U8, name="w_scales", align_bytes=64)
+            for half in range(2):
+                these = slice(half * HALF, (half + 1) * HALF)
+                nc.vector.quantize_mx(
+                    out=w_codes[:, these].rearrange("p u o -> p (u o)").bitcast(FP8X4),
+                    scales=w_scales[:, these].rearrange("p u o -> p (u o)"),
+                    in_=grouped[n][half][:].rearrange("p u o t -> p (u o t)"),
+                )
+            quantised[n] = (w_codes, w_scales)
+
+        load_weights(0)
+        load_weights(1)
+
+        x_t = const.tile([P, IMG, CLASSES, PADDED, BATCH], BF16, name="x_t")
+        nc.vector.memset(x_t[:, :, :, 0, :], 0.0)
+        nc.vector.memset(x_t[:, :, :, PADDED - 1, :], 0.0)
+        zero_row = const.tile([P, CLASSES * BATCH * PACK], BF16, name="zero_row", align_bytes=64)
+        nc.vector.memset(zero_row[:], 0.0)
+        identity = const.tile([P, P], BF16, name="identity")
+        masks.make_identity(nc, identity[:])
+        bias_all = const.tile([P, OUT_HW, OUT_HW, C_OUT], BF16, name="bias_all")
+        pooled = const.tile([P, C_OUT, 4], F32, name="pooled")
+
+        with tc.tile_pool(name="x_stage", bufs=1) as x_pool, tc.psum_pool(name="xt_psum", bufs=4) as xt_psum:
+            x_chunks = x.rearrange("b (k c) h w -> k b (c h w)", k=X_CHUNKS)
+            x_rows = []
+            for k in range(X_CHUNKS):
+                x_rows.append(x_pool.tile([P, V_CHUNK, CLASSES, 2, PIXELS], BF16, name="x_rows%d" % k))
+                nc.sync.dma_start(out=x_rows[k][:].rearrange("b v s e q -> b (v s e q)"), in_=x_chunks[k])
+            load_weights(2)
+            nc.sync.dma_start(
+                out=bias_all[:].rearrange("p a b o -> p (a b o)"),
+                in_=bias.rearrange("l o -> (l o)").partition_broadcast(P),
+            )
+            regroup_weights(0)
+            regroup_weights(1)
+            quantise_weights(0)
+
+            x_sorted = x_pool.tile([P, CLASSES, PIXELS, P], BF16, name="x_sorted")
+            for k in range(X_CHUNKS):
+                for s in range(CLASSES):
+                    nc.vector.tensor_copy(
+                        out=x_sorted[:, s, :, 2 * V_CHUNK * k : 2 * V_CHUNK * (k + 1)].rearrange(
+                            "b q (v e) -> b q v e", e=2
+                        ),
+                        in_=x_rows[k][:, :, s].rearrange("b v e q -> b q v e"),
+                    )
+            for s in range(CLASSES):
+                for r in range(IMG):
+                    flipped = xt_psum.tile([P, IMG, BATCH], BF16, name="flipped")
+                    for col in range(IMG):
+                        nc.tensor.transpose(flipped[:, col, :], x_sorted[:, s, r * IMG + col, :], identity[:])
+                    nc.scalar.copy(out=x_t[:, r, s, 1 : 1 + IMG, :], in_=flipped[:])
+
+        window_pool = ctx.enter_context(tc.tile_pool(name="windows", bufs=2))
+        windows = {}
+
+        def new_windows(ow):
+            windows[ow] = window_pool.tile(
+                [P, IMG, CLASSES, BATCH, PACK], BF16, name="windows", align_bytes=64
+            )
+
+        def regroup_windows(copy, ow, s):
+            regroup(copy, windows[ow][:, :, s], x_t[:, :, s, ow : ow + KER, :])
+
+        new_windows(0)
+        for s in range(CLASSES):
+            regroup_windows(nc.vector.tensor_copy if s < CLASSES // 2 else nc.scalar.copy, 0, s)
+
+        sums = [
+            acc_pool.tile([P, 2, 2, C_OUT], F32, name="sums%d" % w) for w in range(4)
+        ]
+
+        for n in range(len(positions)):
+            oh, ow = positions[n]
+            if n + 2 < len(positions):
+                regroup_weights(n + 2)
+            if ow + 1 < OUT_HW:
+                if oh == 0:
+                    new_windows(ow + 1)
+                regroup_windows(nc.scalar.copy, ow + 1, oh)
+
+            if n + 1 < len(positions):
+                quantise_weights(n + 1)
+            w_codes, w_scales = quantised[n]
+            p_codes = codes_pool.tile([P, KER, CLASSES, BATCH], U32, name="p_codes", align_bytes=64)
+            p_scales = codes_pool.tile([P, KER, CLASSES, BATCH], U8, name="p_scales", align_bytes=64)
+            for i in range(KER):
+                r = oh + i - 1
+                if 0 <= r < IMG:
+                    image_row = windows[ow][:, r].rearrange("p s b t -> p (s b t)")
+                else:
+                    image_row = zero_row[:]
+                nc.vector.quantize_mx(
+                    out=p_codes[:, i].rearrange("p s b -> p (s b)").bitcast(FP8X4),
+                    scales=p_scales[:, i].rearrange("p s b -> p (s b)"),
+                    in_=image_row,
+                )
+
+            window = (oh // 2) * 2 + ow // 2
+            for s in range(CLASSES):
+                for i in range(KER):
+                    nc.tensor.matmul_mx(
+                        out=sums[window][:, oh % 2, ow % 2, :],
+                        lhsT=p_codes[:, i, s, :].bitcast(FP8X4),
+                        lhsT_scale=p_scales[:, i, s, :],
+                        rhs=w_codes[:, s * KER + i, :].bitcast(FP8X4),
+                        rhs_scale=w_scales[:, s * KER + i, :],
+                        start=(s == 0 and i == 0),
+                        stop=(s == CLASSES - 1 and i == KER - 1),
+                    )
+
+            if oh % 2 == 1 and ow % 2 == 1:
+                biased = work.tile([P, 2, 2, C_OUT], F32, name="biased")
+                nc.vector.tensor_tensor(
+                    out=biased[:],
+                    in0=sums[window][:],
+                    in1=bias_all[:, oh - 1 : oh + 1, ow - 1 : ow + 1, :],
+                    op=ADD,
+                )
+                row_max = work.tile([P, 2, C_OUT], F32, name="row_max")
+                nc.vector.tensor_tensor(out=row_max[:], in0=biased[:, 0], in1=biased[:, 1], op=MAX)
+                nc.vector.scalar_tensor_tensor(
+                    out=pooled[:, :, window],
+                    in0=row_max[:, 0, :],
+                    scalar=0.0,
+                    in1=row_max[:, 1, :],
+                    op0=MAX,
+                    op1=MAX,
+                )
+
+        nc.sync.dma_start(
+            out=out.rearrange("b o h w -> b (o h w)"),
+            in_=pooled[:].rearrange("p o w -> p (o w)"),
+        )

@@ -13,6 +13,7 @@ ADD = mybir.AluOpType.add
 
 P = 128
 PACK = 4
+RUN = 4
 BATCH = 128
 C_OUT = 128
 IMG = 5
@@ -31,7 +32,10 @@ FLOPS = 2 * BATCH * (512 * KER * KER) * C_OUT * OUT_HW * OUT_HW
 
 
 def regroup(copy, grouped, rows):
-    copy(out=grouped, in_=rows.rearrange("p u t c -> p u c t"))
+    copy(
+        out=grouped.rearrange("p u (c n) t -> p u c t n", n=RUN),
+        in_=rows.rearrange("p u t (c n) -> p u c t n", n=RUN),
+    )
 
 
 def tile_normalizedlocalmapping_k_kernel(tc, x, weight, bias, out):

@@ -42,12 +42,16 @@ def tile_normalizedlocalmapping_k_kernel(tc, x, weight, bias, out):
     nc = tc.nc
     positions = [(oh, ow) for ow in range(OUT_HW) for oh in range(OUT_HW)]
 
+    def image_copy(s):
+        return nc.vector.tensor_copy if s < CLASSES - 1 else nc.scalar.copy
+
     with ExitStack() as ctx:
         const = ctx.enter_context(tc.tile_pool(name="const", bufs=1))
         raw_pool = ctx.enter_context(tc.tile_pool(name="raw", bufs=RAW_BUFS))
         grouped_pool = ctx.enter_context(tc.tile_pool(name="grouped", bufs=2))
-        codes_pool = ctx.enter_context(tc.tile_pool(name="codes", bufs=2))
-        work = ctx.enter_context(tc.tile_pool(name="work", bufs=2))
+        w_pool = ctx.enter_context(tc.tile_pool(name="w_codes", bufs=3))
+        p_pool = ctx.enter_context(tc.tile_pool(name="p_codes", bufs=2))
+        work = ctx.enter_context(tc.tile_pool(name="work", bufs=1))
         acc_pool = ctx.enter_context(tc.psum_pool(name="acc", bufs=1))
 
         raw = {}
@@ -57,27 +61,34 @@ def tile_normalizedlocalmapping_k_kernel(tc, x, weight, bias, out):
         def load_weights(n):
             oh, ow = positions[n]
             rows = weight[oh * OUT_HW + ow].rearrange(
-                "(v s e k) o -> e v s (k o)", s=CLASSES, e=2, k=KER * KER
+                "(v s e k) o -> s e v (k o)", s=CLASSES, e=2, k=KER * KER
             )
             raw[n] = raw_pool.tile([P, PASSES, PACK, C_OUT], BF16, name="raw")
-            for e in range(2):
-                nc.sync.dma_start(
-                    out=raw[n][e:P:2].rearrange("p (s i) t o -> p s (i t o)", s=CLASSES),
-                    in_=rows[e],
-                )
+            for s in range(CLASSES):
+                for e in range(2):
+                    nc.sync.dma_start(
+                        out=raw[n][e:P:2, s * KER : (s + 1) * KER].rearrange("p i t o -> p (i t o)"),
+                        in_=rows[s, e],
+                    )
 
         def regroup_weights(n):
-            by_vector = grouped_pool.tile([P, HALF, C_OUT, PACK], BF16, name="by_vector", align_bytes=64)
-            by_scalar = grouped_pool.tile([P, HALF, C_OUT, PACK], BF16, name="by_scalar", align_bytes=64)
-            regroup(nc.vector.tensor_copy, by_vector[:], raw[n][:, 0:HALF])
-            regroup(nc.scalar.copy, by_scalar[:], raw[n][:, HALF:PASSES])
-            grouped[n] = (by_vector, by_scalar)
+            halves = []
+            for half in range(2):
+                halves.append(
+                    grouped_pool.tile([P, HALF, C_OUT, PACK], BF16, name="half%d" % half, align_bytes=64)
+                )
+                regroup(
+                    nc.vector.tensor_copy if half == 0 else nc.scalar.copy,
+                    halves[half][:],
+                    raw[n][:, half * HALF : (half + 1) * HALF],
+                )
+            grouped[n] = halves
             if n + RAW_BUFS < len(positions):
                 load_weights(n + RAW_BUFS)
 
         def quantise_weights(n):
-            w_codes = codes_pool.tile([P, PASSES, C_OUT], U32, name="w_codes", align_bytes=64)
-            w_scales = codes_pool.tile([P, PASSES, C_OUT], U8, name="w_scales", align_bytes=64)
+            w_codes = w_pool.tile([P, PASSES, C_OUT], U32, name="w_codes", align_bytes=64)
+            w_scales = w_pool.tile([P, PASSES, C_OUT], U8, name="w_scales", align_bytes=64)
             for half in range(2):
                 these = slice(half * HALF, (half + 1) * HALF)
                 nc.vector.quantize_mx(
@@ -86,9 +97,6 @@ def tile_normalizedlocalmapping_k_kernel(tc, x, weight, bias, out):
                     in_=grouped[n][half][:].rearrange("p u o t -> p (u o t)"),
                 )
             quantised[n] = (w_codes, w_scales)
-
-        load_weights(0)
-        load_weights(1)
 
         x_t = const.tile([P, IMG, CLASSES, PADDED, BATCH], BF16, name="x_t")
         nc.vector.memset(x_t[:, :, :, 0, :], 0.0)
@@ -106,19 +114,17 @@ def tile_normalizedlocalmapping_k_kernel(tc, x, weight, bias, out):
             for k in range(X_CHUNKS):
                 x_rows.append(x_pool.tile([P, V_CHUNK, CLASSES, 2, PIXELS], BF16, name="x_rows%d" % k))
                 nc.sync.dma_start(out=x_rows[k][:].rearrange("b v s e q -> b (v s e q)"), in_=x_chunks[k])
-            load_weights(2)
+            for n in range(RAW_BUFS):
+                load_weights(n)
             nc.sync.dma_start(
                 out=bias_all[:].rearrange("p a b o -> p (a b o)"),
                 in_=bias.rearrange("l o -> (l o)").partition_broadcast(P),
             )
-            regroup_weights(0)
-            regroup_weights(1)
-            quantise_weights(0)
 
             x_sorted = x_pool.tile([P, CLASSES, PIXELS, P], BF16, name="x_sorted")
             for k in range(X_CHUNKS):
                 for s in range(CLASSES):
-                    nc.vector.tensor_copy(
+                    image_copy(s)(
                         out=x_sorted[:, s, :, 2 * V_CHUNK * k : 2 * V_CHUNK * (k + 1)].rearrange(
                             "b q (v e) -> b q v e", e=2
                         ),
@@ -142,14 +148,35 @@ def tile_normalizedlocalmapping_k_kernel(tc, x, weight, bias, out):
         def regroup_windows(copy, ow, s):
             regroup(copy, windows[ow][:, :, s], x_t[:, :, s, ow : ow + KER, :])
 
+        regroup_weights(0)
         new_windows(0)
         for s in range(CLASSES):
-            regroup_windows(nc.vector.tensor_copy if s < CLASSES // 2 else nc.scalar.copy, 0, s)
+            regroup_windows(image_copy(s), 0, s)
+        regroup_weights(1)
+        quantise_weights(0)
 
-        sums = [
-            acc_pool.tile([P, 2, 2, C_OUT], F32, name="sums%d" % w) for w in range(4)
-        ]
+        sums = [acc_pool.tile([P, 2, 2, C_OUT], F32, name="sums%d" % w) for w in range(4)]
 
+        def pool_window(ph, pw):
+            biased = work.tile([P, 2, 2, C_OUT], F32, name="biased")
+            nc.vector.tensor_tensor(
+                out=biased[:],
+                in0=sums[ph * 2 + pw][:],
+                in1=bias_all[:, 2 * ph : 2 * ph + 2, 2 * pw : 2 * pw + 2, :],
+                op=ADD,
+            )
+            row_max = work.tile([P, 2, C_OUT], F32, name="row_max")
+            nc.vector.tensor_tensor(out=row_max[:], in0=biased[:, 0], in1=biased[:, 1], op=MAX)
+            nc.vector.scalar_tensor_tensor(
+                out=pooled[:, :, ph * 2 + pw],
+                in0=row_max[:, 0, :],
+                scalar=0.0,
+                in1=row_max[:, 1, :],
+                op0=MAX,
+                op1=MAX,
+            )
+
+        complete = []
         for n in range(len(positions)):
             oh, ow = positions[n]
             if n + 2 < len(positions):
@@ -158,12 +185,11 @@ def tile_normalizedlocalmapping_k_kernel(tc, x, weight, bias, out):
                 if oh == 0:
                     new_windows(ow + 1)
                 regroup_windows(nc.scalar.copy, ow + 1, oh)
-
             if n + 1 < len(positions):
                 quantise_weights(n + 1)
-            w_codes, w_scales = quantised[n]
-            p_codes = codes_pool.tile([P, KER, CLASSES, BATCH], U32, name="p_codes", align_bytes=64)
-            p_scales = codes_pool.tile([P, KER, CLASSES, BATCH], U8, name="p_scales", align_bytes=64)
+
+            p_codes = p_pool.tile([P, KER, CLASSES, BATCH], U32, name="p_codes", align_bytes=64)
+            p_scales = p_pool.tile([P, KER, CLASSES, BATCH], U8, name="p_scales", align_bytes=64)
             for i in range(KER):
                 r = oh + i - 1
                 if 0 <= r < IMG:
@@ -176,38 +202,27 @@ def tile_normalizedlocalmapping_k_kernel(tc, x, weight, bias, out):
                     in_=image_row,
                 )
 
-            window = (oh // 2) * 2 + ow // 2
-            for s in range(CLASSES):
-                for i in range(KER):
+            for ph, pw in complete:
+                pool_window(ph, pw)
+            complete = []
+
+            w_codes, w_scales = quantised[n]
+            for i in range(KER):
+                for s in range(CLASSES):
                     nc.tensor.matmul_mx(
-                        out=sums[window][:, oh % 2, ow % 2, :],
+                        out=sums[(oh // 2) * 2 + ow // 2][:, oh % 2, ow % 2, :],
                         lhsT=p_codes[:, i, s, :].bitcast(FP8X4),
                         lhsT_scale=p_scales[:, i, s, :],
                         rhs=w_codes[:, s * KER + i, :].bitcast(FP8X4),
                         rhs_scale=w_scales[:, s * KER + i, :],
-                        start=(s == 0 and i == 0),
-                        stop=(s == CLASSES - 1 and i == KER - 1),
+                        start=(i == 0 and s == 0),
+                        stop=(i == KER - 1 and s == CLASSES - 1),
                     )
-
             if oh % 2 == 1 and ow % 2 == 1:
-                biased = work.tile([P, 2, 2, C_OUT], F32, name="biased")
-                nc.vector.tensor_tensor(
-                    out=biased[:],
-                    in0=sums[window][:],
-                    in1=bias_all[:, oh - 1 : oh + 1, ow - 1 : ow + 1, :],
-                    op=ADD,
-                )
-                row_max = work.tile([P, 2, C_OUT], F32, name="row_max")
-                nc.vector.tensor_tensor(out=row_max[:], in0=biased[:, 0], in1=biased[:, 1], op=MAX)
-                nc.vector.scalar_tensor_tensor(
-                    out=pooled[:, :, window],
-                    in0=row_max[:, 0, :],
-                    scalar=0.0,
-                    in1=row_max[:, 1, :],
-                    op0=MAX,
-                    op1=MAX,
-                )
+                complete.append((oh // 2, ow // 2))
 
+        for ph, pw in complete:
+            pool_window(ph, pw)
         nc.sync.dma_start(
             out=out.rearrange("b o h w -> b (o h w)"),
             in_=pooled[:].rearrange("p o w -> p (o w)"),

@@ -46,6 +46,7 @@ def tile_normalizedlocalmapping_k_kernel(tc, x, weight, bias, out):
         return nc.vector.tensor_copy if s < CLASSES - 1 else nc.scalar.copy
 
     with ExitStack() as ctx:
+        ctx.enter_context(tc.manual_schedule())
         const = ctx.enter_context(tc.tile_pool(name="const", bufs=1))
         raw_pool = ctx.enter_context(tc.tile_pool(name="raw", bufs=RAW_BUFS))
         grouped_pool = ctx.enter_context(tc.tile_pool(name="grouped", bufs=2))

@@ -131,12 +131,23 @@ def tile_normalizedlocalmapping_k_kernel(tc, x, weight, bias, out):
                         ),
                         in_=x_rows[k][:, :, s].rearrange("b v e q -> b q v e"),
                     )
-            for s in range(CLASSES):
+
+            def transpose_class(s):
                 for r in range(IMG):
                     flipped = xt_psum.tile([P, IMG, BATCH], BF16, name="flipped")
                     for col in range(IMG):
                         nc.tensor.transpose(flipped[:, col, :], x_sorted[:, s, r * IMG + col, :], identity[:])
-                    nc.scalar.copy(out=x_t[:, r, s, 1 : 1 + IMG, :], in_=flipped[:])
+                    image_copy(s)(out=x_t[:, r, s, 1 : 1 + IMG, :], in_=flipped[:])
+
+            regroup_weights(0)
+            transpose_class(0)
+            regroup_weights(1)
+            transpose_class(1)
+            quantise_weights(0)
+            transpose_class(2)
+            regroup_weights(2)
+            transpose_class(3)
+            quantise_weights(1)
 
         window_pool = ctx.enter_context(tc.tile_pool(name="windows", bufs=2))
         windows = {}
@@ -149,12 +160,9 @@ def tile_normalizedlocalmapping_k_kernel(tc, x, weight, bias, out):
         def regroup_windows(copy, ow, s):
             regroup(copy, windows[ow][:, :, s], x_t[:, :, s, ow : ow + KER, :])
 
-        regroup_weights(0)
         new_windows(0)
         for s in range(CLASSES):
             regroup_windows(image_copy(s), 0, s)
-        regroup_weights(1)
-        quantise_weights(0)
 
         sums = [acc_pool.tile([P, 2, 2, C_OUT], F32, name="sums%d" % w) for w in range(4)]
 
@@ -180,14 +188,12 @@ def tile_normalizedlocalmapping_k_kernel(tc, x, weight, bias, out):
         complete = []
         for n in range(len(positions)):
             oh, ow = positions[n]
-            if n + 2 < len(positions):
-                regroup_weights(n + 2)
+            if n + 3 < len(positions):
+                regroup_weights(n + 3)
             if ow + 1 < OUT_HW:
                 if oh == 0:
                     new_windows(ow + 1)
                 regroup_windows(nc.scalar.copy, ow + 1, oh)
-            if n + 1 < len(positions):
-                quantise_weights(n + 1)
 
             p_codes = p_pool.tile([P, KER, CLASSES, BATCH], U32, name="p_codes", align_bytes=64)
             p_scales = p_pool.tile([P, KER, CLASSES, BATCH], U8, name="p_scales", align_bytes=64)
@@ -221,6 +227,8 @@ def tile_normalizedlocalmapping_k_kernel(tc, x, weight, bias, out):
                     )
             if oh % 2 == 1 and ow % 2 == 1:
                 complete.append((oh // 2, ow // 2))
+            if n + 2 < len(positions):
+                quantise_weights(n + 2)
 
         for ph, pw in complete:
             pool_window(ph, pw)

@@ -17,16 +17,17 @@ RUN = 4
 BATCH = 128
 C_OUT = 128
 IMG = 5
-PADDED = IMG + 2
 KER = 4
 OUT_HW = 4
 CLASSES = 4
 PASSES = CLASSES * KER
 HALF = PASSES // 2
 PIXELS = IMG * IMG
-X_CHUNKS = 4
+X_CHUNKS = 2
 V_CHUNK = 64 // X_CHUNKS
+PAIRS = 3
 RAW_BUFS = 3
+AHEAD = 2
 
 FLOPS = 2 * BATCH * (512 * KER * KER) * C_OUT * OUT_HW * OUT_HW
 
@@ -42,127 +43,149 @@ def tile_normalizedlocalmapping_k_kernel(tc, x, weight, bias, out):
     nc = tc.nc
     positions = [(oh, ow) for ow in range(OUT_HW) for oh in range(OUT_HW)]
 
-    def image_copy(s):
-        return nc.vector.tensor_copy if s < CLASSES - 1 else nc.scalar.copy
-
     with ExitStack() as ctx:
         ctx.enter_context(tc.manual_schedule())
         const = ctx.enter_context(tc.tile_pool(name="const", bufs=1))
         raw_pool = ctx.enter_context(tc.tile_pool(name="raw", bufs=RAW_BUFS))
         grouped_pool = ctx.enter_context(tc.tile_pool(name="grouped", bufs=2))
-        w_pool = ctx.enter_context(tc.tile_pool(name="w_codes", bufs=3))
+        w_pool = ctx.enter_context(tc.tile_pool(name="w_codes", bufs=2))
         p_pool = ctx.enter_context(tc.tile_pool(name="p_codes", bufs=2))
+        window_pool = ctx.enter_context(tc.tile_pool(name="windows", bufs=2))
         work = ctx.enter_context(tc.tile_pool(name="work", bufs=1))
         acc_pool = ctx.enter_context(tc.psum_pool(name="acc", bufs=1))
+        flip_pool = ctx.enter_context(tc.psum_pool(name="flip", bufs=4))
 
         raw = {}
         grouped = {}
         quantised = {}
 
-        def load_weights(n):
+        def load_classes(n, classes):
             oh, ow = positions[n]
             rows = weight[oh * OUT_HW + ow].rearrange(
                 "(v s e k) o -> s e v (k o)", s=CLASSES, e=2, k=KER * KER
             )
-            raw[n] = raw_pool.tile([P, PASSES, PACK, C_OUT], BF16, name="raw")
-            for s in range(CLASSES):
+            if n not in raw:
+                raw[n] = raw_pool.tile([P, PASSES, PACK, C_OUT], BF16, name="raw")
+            for s in classes:
                 for e in range(2):
                     nc.sync.dma_start(
                         out=raw[n][e:P:2, s * KER : (s + 1) * KER].rearrange("p i t o -> p (i t o)"),
                         in_=rows[s, e],
                     )
 
-        def regroup_weights(n):
-            halves = []
-            for half in range(2):
-                halves.append(
-                    grouped_pool.tile([P, HALF, C_OUT, PACK], BF16, name="half%d" % half, align_bytes=64)
-                )
-                regroup(
-                    nc.vector.tensor_copy if half == 0 else nc.scalar.copy,
-                    halves[half][:],
-                    raw[n][:, half * HALF : (half + 1) * HALF],
-                )
-            grouped[n] = halves
+        def regroup_half(n, half):
+            by_vector = half == 0 and n < len(positions) - 1
+            grouped[n, half] = grouped_pool.tile(
+                [P, HALF, C_OUT, PACK], BF16, name="half%d" % half, align_bytes=64
+            )
+            regroup(
+                nc.vector.tensor_copy if by_vector else nc.scalar.copy,
+                grouped[n, half][:],
+                raw[n][:, half * HALF : (half + 1) * HALF],
+            )
             if n + RAW_BUFS < len(positions):
-                load_weights(n + RAW_BUFS)
+                load_classes(n + RAW_BUFS, (2 * half, 2 * half + 1))
 
-        def quantise_weights(n):
-            w_codes = w_pool.tile([P, PASSES, C_OUT], U32, name="w_codes", align_bytes=64)
-            w_scales = w_pool.tile([P, PASSES, C_OUT], U8, name="w_scales", align_bytes=64)
-            for half in range(2):
-                these = slice(half * HALF, (half + 1) * HALF)
-                nc.vector.quantize_mx(
-                    out=w_codes[:, these].rearrange("p u o -> p (u o)").bitcast(FP8X4),
-                    scales=w_scales[:, these].rearrange("p u o -> p (u o)"),
-                    in_=grouped[n][half][:].rearrange("p u o t -> p (u o t)"),
-                )
-            quantised[n] = (w_codes, w_scales)
+        def quantise_half(n, half):
+            w_codes = w_pool.tile([P, HALF, C_OUT], U32, name="w_codes%d" % half, align_bytes=64)
+            w_scales = w_pool.tile([P, HALF, C_OUT], U8, name="w_scales%d" % half, align_bytes=64)
+            nc.vector.quantize_mx(
+                out=w_codes[:].rearrange("p u o -> p (u o)").bitcast(FP8X4),
+                scales=w_scales[:].rearrange("p u o -> p (u o)"),
+                in_=grouped[n, half][:].rearrange("p u o t -> p (u o t)"),
+            )
+            quantised[n, half] = (w_codes, w_scales)
 
-        x_t = const.tile([P, IMG, CLASSES, PADDED, BATCH], BF16, name="x_t")
-        nc.vector.memset(x_t[:, :, :, 0, :], 0.0)
-        nc.vector.memset(x_t[:, :, :, PADDED - 1, :], 0.0)
+        x_pairs = const.tile([P, CLASSES, IMG, PAIRS, P, 2], BF16, name="x_pairs")
+        nc.gpsimd.memset(
+            x_pairs[:, :, :, 0].rearrange("b s r p j -> b (s r) (p j)").bitcast(U32), 0
+        )
+        identity = const.tile([P, P], F32, name="identity")
+        masks.make_identity(nc, identity[:])
         zero_row = const.tile([P, CLASSES * BATCH * PACK], BF16, name="zero_row", align_bytes=64)
         nc.vector.memset(zero_row[:], 0.0)
-        identity = const.tile([P, P], BF16, name="identity")
-        masks.make_identity(nc, identity[:])
+        first_copy = const.tile([P, 2], BF16, name="first_copy")
+        nc.scalar.copy(out=first_copy[:], in_=zero_row[:, 0:2])
+        zero_words = zero_row[:, 0 : 2 * P].bitcast(F32)
         bias_all = const.tile([P, OUT_HW, OUT_HW, C_OUT], BF16, name="bias_all")
         pooled = const.tile([P, C_OUT, 4], F32, name="pooled")
 
-        with tc.tile_pool(name="x_stage", bufs=1) as x_pool, tc.psum_pool(name="xt_psum", bufs=4) as xt_psum:
+        with tc.tile_pool(name="x_stage", bufs=1) as x_pool:
             x_chunks = x.rearrange("b (k c) h w -> k b (c h w)", k=X_CHUNKS)
             x_rows = []
             for k in range(X_CHUNKS):
                 x_rows.append(x_pool.tile([P, V_CHUNK, CLASSES, 2, PIXELS], BF16, name="x_rows%d" % k))
-                nc.sync.dma_start(out=x_rows[k][:].rearrange("b v s e q -> b (v s e q)"), in_=x_chunks[k])
-            for n in range(RAW_BUFS):
-                load_weights(n)
-            nc.sync.dma_start(
-                out=bias_all[:].rearrange("p a b o -> p (a b o)"),
-                in_=bias.rearrange("l o -> (l o)").partition_broadcast(P),
-            )
 
-            x_sorted = x_pool.tile([P, CLASSES, PIXELS, P], BF16, name="x_sorted")
-            for k in range(X_CHUNKS):
+            def load_image(k):
+                nc.sync.dma_start(out=x_rows[k][:].rearrange("b v s e q -> b (v s e q)"), in_=x_chunks[k])
+
+            load_classes(0, range(CLASSES))
+            load_image(0)
+            load_image(1)
+            load_classes(1, range(CLASSES))
+            load_classes(2, range(CLASSES))
+
+            def sort_image(k):
                 for s in range(CLASSES):
-                    image_copy(s)(
-                        out=x_sorted[:, s, :, 2 * V_CHUNK * k : 2 * V_CHUNK * (k + 1)].rearrange(
-                            "b q (v e) -> b q v e", e=2
-                        ),
-                        in_=x_rows[k][:, :, s].rearrange("b v e q -> b q v e"),
+                    mine = slice(2 * V_CHUNK * k, 2 * V_CHUNK * (k + 1))
+                    pairs = x_pairs[:, s, :, :, mine].rearrange("b r w (v e) j -> b r w v e j", e=2)
+                    pixels = x_rows[k][:, :, s].rearrange("b v e (r c) -> b r v e c", c=IMG)
+                    nc.scalar.copy(out=pairs[:, :, 0, :, :, 1], in_=pixels[:, :, :, :, 0])
+                    for w in range(1, PAIRS):
+                        nc.vector.tensor_copy(
+                            out=pairs[:, 0 : IMG - 1, w], in_=pixels[:, 0 : IMG - 1, :, :, 2 * w - 1 : 2 * w + 1]
+                        )
+                    nc.vector.tensor_copy(
+                        out=pairs[:, IMG - 1, 1:PAIRS],
+                        in_=pixels[:, IMG - 1, :, :, 1:IMG].rearrange("b v e (w j) -> b w v e j", j=2),
                     )
 
-            def transpose_class(s):
-                for r in range(IMG):
-                    flipped = xt_psum.tile([P, IMG, BATCH], BF16, name="flipped")
-                    for col in range(IMG):
-                        nc.tensor.transpose(flipped[:, col, :], x_sorted[:, s, r * IMG + col, :], identity[:])
-                    image_copy(s)(out=x_t[:, r, s, 1 : 1 + IMG, :], in_=flipped[:])
+            regroup_half(0, 0)
+            regroup_half(0, 1)
+            sort_image(0)
+            quantise_half(0, 0)
+            sort_image(1)
 
-            regroup_weights(0)
-            transpose_class(0)
-            regroup_weights(1)
-            transpose_class(1)
-            quantise_weights(0)
-            transpose_class(2)
-            regroup_weights(2)
-            transpose_class(3)
-            quantise_weights(1)
-
-        window_pool = ctx.enter_context(tc.tile_pool(name="windows", bufs=2))
         windows = {}
 
+        def flip_jobs(ow):
+            step = 2 if ow % 2 == 0 else 1
+            return [(r, list(range(s, s + step))) for r in range(IMG) for s in range(0, CLASSES, step)]
+
+        def flip(ow, r, classes):
+            pairs = list(range(ow // 2, ow // 2 + (2 if ow % 2 == 0 else 3)))
+            flipped = flip_pool.tile([P, len(classes), BATCH, len(pairs)], F32, name="flipped")
+            for a in range(len(classes)):
+                for h in range(len(pairs)):
+                    if pairs[h] < PAIRS:
+                        words = x_pairs[:, classes[a], r, pairs[h]].rearrange("b p j -> b (p j)").bitcast(F32)
+                    else:
+                        words = zero_words
+                    nc.tensor.transpose(flipped[:, a, :, h], words, identity[:])
+            return flipped
+
+        def unload(copy, ow, r, classes, flipped):
+            target = windows[ow][:, r, classes[0] : classes[-1] + 1]
+            if ow % 2 == 0:
+                copy(
+                    out=target.rearrange("p s b t -> p (s b t)").bitcast(F32),
+                    in_=flipped[:].rearrange("p s b h -> p (s b h)"),
+                )
+            else:
+                columns = flipped[:].rearrange("p s b h -> p (s b h)").bitcast(BF16)
+                copy(
+                    out=target.rearrange("p s b t -> p (s b) t"),
+                    in_=columns.rearrange("p (b k) -> p b k", k=6)[:, :, 1:5],
+                )
+
         def new_windows(ow):
-            windows[ow] = window_pool.tile(
-                [P, IMG, CLASSES, BATCH, PACK], BF16, name="windows", align_bytes=64
-            )
+            windows[ow] = window_pool.tile([P, IMG, CLASSES, BATCH, PACK], BF16, name="windows", align_bytes=64)
 
-        def regroup_windows(copy, ow, s):
-            regroup(copy, windows[ow][:, :, s], x_t[:, :, s, ow : ow + KER, :])
-
+        regroup_half(1, 0)
         new_windows(0)
-        for s in range(CLASSES):
-            regroup_windows(image_copy(s), 0, s)
+        for r, classes in flip_jobs(0):
+            unload(nc.scalar.copy if classes[0] == 0 else nc.vector.tensor_copy, 0, r, classes, flip(0, r, classes))
+        regroup_half(1, 1)
 
         sums = [acc_pool.tile([P, 2, 2, C_OUT], F32, name="sums%d" % w) for w in range(4)]
 
@@ -188,47 +211,64 @@ def tile_normalizedlocalmapping_k_kernel(tc, x, weight, bias, out):
         complete = []
         for n in range(len(positions)):
             oh, ow = positions[n]
-            if n + 3 < len(positions):
-                regroup_weights(n + 3)
-            if ow + 1 < OUT_HW:
+            if n + AHEAD < len(positions):
+                regroup_half(n + AHEAD, 0)
+            if n == 1:
+                nc.sync.dma_start(
+                    out=bias_all[:].rearrange("p a b o -> p (a b o)"),
+                    in_=bias.rearrange("l o -> (l o)").partition_broadcast(P),
+                )
+            if ow + 1 < OUT_HW and oh < 3:
                 if oh == 0:
                     new_windows(ow + 1)
-                regroup_windows(nc.scalar.copy, ow + 1, oh)
+                jobs = flip_jobs(ow + 1)
+                for r, classes in jobs[oh * len(jobs) // 3 : (oh + 1) * len(jobs) // 3]:
+                    unload(nc.scalar.copy, ow + 1, r, classes, flip(ow + 1, r, classes))
 
             p_codes = p_pool.tile([P, KER, CLASSES, BATCH], U32, name="p_codes", align_bytes=64)
             p_scales = p_pool.tile([P, KER, CLASSES, BATCH], U8, name="p_scales", align_bytes=64)
-            for i in range(KER):
-                r = oh + i - 1
+            if oh == 0:
+                groups = [(0, 1), (1, 3), (3, 4)]
+            elif oh == OUT_HW - 1:
+                groups = [(0, 2), (2, 3), (3, 4)]
+            else:
+                groups = [(0, 2), (2, 4)]
+            for a, z in groups:
+                r = oh + a - 1
                 if 0 <= r < IMG:
-                    image_row = windows[ow][:, r].rearrange("p s b t -> p (s b t)")
+                    image_rows = windows[ow][:, r : r + z - a].rearrange("p i s b t -> p (i s b t)")
                 else:
-                    image_row = zero_row[:]
+                    image_rows = zero_row[:]
                 nc.vector.quantize_mx(
-                    out=p_codes[:, i].rearrange("p s b -> p (s b)").bitcast(FP8X4),
-                    scales=p_scales[:, i].rearrange("p s b -> p (s b)"),
-                    in_=image_row,
+                    out=p_codes[:, a:z].rearrange("p i s b -> p (i s b)").bitcast(FP8X4),
+                    scales=p_scales[:, a:z].rearrange("p i s b -> p (i s b)"),
+                    in_=image_rows,
                 )
+
+            quantise_half(n, 1)
+            if n + AHEAD < len(positions):
+                regroup_half(n + AHEAD, 1)
 
             for ph, pw in complete:
                 pool_window(ph, pw)
             complete = []
 
-            w_codes, w_scales = quantised[n]
-            for i in range(KER):
-                for s in range(CLASSES):
-                    nc.tensor.matmul_mx(
-                        out=sums[(oh // 2) * 2 + ow // 2][:, oh % 2, ow % 2, :],
-                        lhsT=p_codes[:, i, s, :].bitcast(FP8X4),
-                        lhsT_scale=p_scales[:, i, s, :],
-                        rhs=w_codes[:, s * KER + i, :].bitcast(FP8X4),
-                        rhs_scale=w_scales[:, s * KER + i, :],
-                        start=(i == 0 and s == 0),
-                        stop=(i == KER - 1 and s == CLASSES - 1),
-                    )
+            for u in range(PASSES):
+                half, i, s = u // HALF, u % HALF // 2, u // HALF * 2 + u % 2
+                w_codes, w_scales = quantised[n, half]
+                nc.tensor.matmul_mx(
+                    out=sums[(oh // 2) * 2 + ow // 2][:, oh % 2, ow % 2, :],
+                    lhsT=p_codes[:, i, s, :].bitcast(FP8X4),
+                    lhsT_scale=p_scales[:, i, s, :],
+                    rhs=w_codes[:, s % 2 * KER + i, :].bitcast(FP8X4),
+                    rhs_scale=w_scales[:, s % 2 * KER + i, :],
+                    start=(u == 0),
+                    stop=(u == PASSES - 1),
+                )
             if oh % 2 == 1 and ow % 2 == 1:
                 complete.append((oh // 2, ow // 2))
-            if n + 2 < len(positions):
-                quantise_weights(n + 2)
+            if n + 1 < len(positions):
+                quantise_half(n + 1, 0)
 
         for ph, pw in complete:
             pool_window(ph, pw)

@@ -22,6 +22,7 @@ OUT_HW = 4
 CLASSES = 4
 PASSES = CLASSES * KER
 HALF = PASSES // 2
+VECTOR_PASSES = 6
 PIXELS = IMG * IMG
 X_CHUNKS = 2
 V_CHUNK = 64 // X_CHUNKS
@@ -74,15 +75,14 @@ def tile_normalizedlocalmapping_k_kernel(tc, x, weight, bias, out):
                     )
 
         def regroup_half(n, half):
-            by_vector = half == 0 and n < len(positions) - 1
             grouped[n, half] = grouped_pool.tile(
                 [P, HALF, C_OUT, PACK], BF16, name="half%d" % half, align_bytes=64
             )
-            regroup(
-                nc.vector.tensor_copy if by_vector else nc.scalar.copy,
-                grouped[n, half][:],
-                raw[n][:, half * HALF : (half + 1) * HALF],
-            )
+            first = VECTOR_PASSES if half == 0 and n < len(positions) - 1 else 0
+            rows = raw[n][:, half * HALF : (half + 1) * HALF]
+            if first > 0:
+                regroup(nc.vector.tensor_copy, grouped[n, half][:, 0:first], rows[:, 0:first])
+            regroup(nc.scalar.copy, grouped[n, half][:, first:HALF], rows[:, first:HALF])
             if n + RAW_BUFS < len(positions):
                 load_classes(n + RAW_BUFS, (2 * half, 2 * half + 1))
 

@@ -53,8 +53,8 @@ def tile_normalizedlocalmapping_k_kernel(tc, x, weight, bias, out):
         p_pool = ctx.enter_context(tc.tile_pool(name="p_codes", bufs=2))
         window_pool = ctx.enter_context(tc.tile_pool(name="windows", bufs=2))
         work = ctx.enter_context(tc.tile_pool(name="work", bufs=1))
-        acc_pool = ctx.enter_context(tc.psum_pool(name="acc", bufs=1))
-        flip_pool = ctx.enter_context(tc.psum_pool(name="flip", bufs=4))
+        acc_pool = ctx.enter_context(tc.psum_pool(name="acc", bufs=3))
+        flip_pool = ctx.enter_context(tc.psum_pool(name="flip", bufs=5))
 
         raw = {}
         grouped = {}
@@ -154,22 +154,28 @@ def tile_normalizedlocalmapping_k_kernel(tc, x, weight, bias, out):
 
         def flip(ow, r, classes):
             pairs = list(range(ow // 2, ow // 2 + (2 if ow % 2 == 0 else 3)))
-            flipped = flip_pool.tile([P, len(classes), BATCH, len(pairs)], F32, name="flipped")
+            if ow % 2 == 0:
+                flipped = flip_pool.tile([P, len(classes), len(pairs), BATCH], F32, name="flipped")
+            else:
+                flipped = flip_pool.tile([P, len(classes), BATCH, len(pairs)], F32, name="flipped")
             for a in range(len(classes)):
                 for h in range(len(pairs)):
                     if pairs[h] < PAIRS:
                         words = x_pairs[:, classes[a], r, pairs[h]].rearrange("b p j -> b (p j)").bitcast(F32)
                     else:
                         words = zero_words
-                    nc.tensor.transpose(flipped[:, a, :, h], words, identity[:])
+                    target = flipped[:, a, h, :] if ow % 2 == 0 else flipped[:, a, :, h]
+                    nc.tensor.transpose(target, words, identity[:])
             return flipped
 
         def unload(copy, ow, r, classes, flipped):
             target = windows[ow][:, r, classes[0] : classes[-1] + 1]
             if ow % 2 == 0:
                 copy(
-                    out=target.rearrange("p s b t -> p (s b t)").bitcast(F32),
-                    in_=flipped[:].rearrange("p s b h -> p (s b h)"),
+                    out=target.rearrange("p s b t -> p (s b t)")
+                    .bitcast(F32)
+                    .rearrange("p (s b h) -> p s b h", s=2, h=2),
+                    in_=flipped[:].rearrange("p s h b -> p s b h"),
                 )
             else:
                 columns = flipped[:].rearrange("p s b h -> p (s b h)").bitcast(BF16)
@@ -187,13 +193,13 @@ def tile_normalizedlocalmapping_k_kernel(tc, x, weight, bias, out):
             unload(nc.scalar.copy if classes[0] == 0 else nc.vector.tensor_copy, 0, r, classes, flip(0, r, classes))
         regroup_half(1, 1)
 
-        sums = [acc_pool.tile([P, 2, 2, C_OUT], F32, name="sums%d" % w) for w in range(4)]
+        sums = {}
 
         def pool_window(ph, pw):
             biased = work.tile([P, 2, 2, C_OUT], F32, name="biased")
             nc.vector.tensor_tensor(
                 out=biased[:],
-                in0=sums[ph * 2 + pw][:],
+                in0=sums[ph, pw][:],
                 in1=bias_all[:, 2 * ph : 2 * ph + 2, 2 * pw : 2 * pw + 2, :],
                 op=ADD,
             )
@@ -208,6 +214,12 @@ def tile_normalizedlocalmapping_k_kernel(tc, x, weight, bias, out):
                 op1=MAX,
             )
 
+        def flip_batch(ow, quarter):
+            jobs = flip_jobs(ow)
+            these = jobs[quarter * len(jobs) // OUT_HW : (quarter + 1) * len(jobs) // OUT_HW]
+            return [(r, classes, flip(ow, r, classes)) for r, classes in these]
+
+        pending = flip_batch(1, 0)
         complete = []
         for n in range(len(positions)):
             oh, ow = positions[n]
@@ -218,12 +230,10 @@ def tile_normalizedlocalmapping_k_kernel(tc, x, weight, bias, out):
                     out=bias_all[:].rearrange("p a b o -> p (a b o)"),
                     in_=bias.rearrange("l o -> (l o)").partition_broadcast(P),
                 )
-            if ow + 1 < OUT_HW and oh < 3:
-                if oh == 0:
-                    new_windows(ow + 1)
-                jobs = flip_jobs(ow + 1)
-                for r, classes in jobs[oh * len(jobs) // 3 : (oh + 1) * len(jobs) // 3]:
-                    unload(nc.scalar.copy, ow + 1, r, classes, flip(ow + 1, r, classes))
+            if oh == 0 and ow + 1 < OUT_HW:
+                new_windows(ow + 1)
+            for r, classes, flipped in pending:
+                unload(nc.scalar.copy, ow + 1, r, classes, flipped)
 
             p_codes = p_pool.tile([P, KER, CLASSES, BATCH], U32, name="p_codes", align_bytes=64)
             p_scales = p_pool.tile([P, KER, CLASSES, BATCH], U8, name="p_scales", align_bytes=64)
@@ -253,11 +263,14 @@ def tile_normalizedlocalmapping_k_kernel(tc, x, weight, bias, out):
                 pool_window(ph, pw)
             complete = []
 
+            window = (oh // 2, ow // 2)
+            if window not in sums:
+                sums[window] = acc_pool.tile([P, 2, 2, C_OUT], F32, name="sums")
             for u in range(PASSES):
                 half, i, s = u // HALF, u % HALF // 2, u // HALF * 2 + u % 2
                 w_codes, w_scales = quantised[n, half]
                 nc.tensor.matmul_mx(
-                    out=sums[(oh // 2) * 2 + ow // 2][:, oh % 2, ow % 2, :],
+                    out=sums[window][:, oh % 2, ow % 2, :],
                     lhsT=p_codes[:, i, s, :].bitcast(FP8X4),
                     lhsT_scale=p_scales[:, i, s, :],
                     rhs=w_codes[:, s % 2 * KER + i, :].bitcast(FP8X4),
@@ -267,6 +280,11 @@ def tile_normalizedlocalmapping_k_kernel(tc, x, weight, bias, out):
                 )
             if oh % 2 == 1 and ow % 2 == 1:
                 complete.append((oh // 2, ow // 2))
+            pending = []
+            if oh + 1 < OUT_HW and ow + 1 < OUT_HW:
+                pending = flip_batch(ow + 1, oh + 1)
+            elif ow + 2 < OUT_HW:
+                pending = flip_batch(ow + 2, 0)
             if n + 1 < len(positions):
                 quantise_half(n + 1, 0)
 

@@ -59,6 +59,7 @@ def tile_normalizedlocalmapping_k_kernel(tc, x, weight, bias, out):
         raw = {}
         grouped = {}
         quantised = {}
+        moved = {}
 
         def load_classes(n, classes):
             oh, ow = positions[n]
@@ -82,9 +83,26 @@ def tile_normalizedlocalmapping_k_kernel(tc, x, weight, bias, out):
             rows = raw[n][:, half * HALF : (half + 1) * HALF]
             if first > 0:
                 regroup(nc.vector.tensor_copy, grouped[n, half][:, 0:first], rows[:, 0:first])
-            regroup(nc.scalar.copy, grouped[n, half][:, first:HALF], rows[:, first:HALF])
+            if half == 0 and n in moved:
+                nc.scalar.copy(
+                    out=grouped[n, half][:, first:HALF].rearrange("p u o t -> p (u o t)"),
+                    in_=moved[n][:].rearrange("p u o t -> p (u o t)"),
+                )
+            else:
+                regroup(nc.scalar.copy, grouped[n, half][:, first:HALF], rows[:, first:HALF])
             if n + RAW_BUFS < len(positions):
                 load_classes(n + RAW_BUFS, (2 * half, 2 * half + 1))
+
+        def move_weights(n):
+            moved[n] = flip_pool.tile([P, HALF - VECTOR_PASSES, C_OUT, PACK], BF16, name="flipped")
+            for u in range(VECTOR_PASSES, HALF):
+                nc.tensor.matmul(
+                    moved[n][:, u - VECTOR_PASSES].rearrange("p o t -> p t o"),
+                    lhsT=identity_bf16[:],
+                    rhs=raw[n][:, u],
+                    start=True,
+                    stop=True,
+                )
 
         def quantise_half(n, half):
             w_codes = w_pool.tile([P, HALF, C_OUT], U32, name="w_codes%d" % half, align_bytes=64)
@@ -102,6 +120,8 @@ def tile_normalizedlocalmapping_k_kernel(tc, x, weight, bias, out):
         )
         identity = const.tile([P, P], F32, name="identity")
         masks.make_identity(nc, identity[:])
+        identity_bf16 = const.tile([P, P], BF16, name="identity_bf16")
+        masks.make_identity(nc, identity_bf16[:])
         zero_row = const.tile([P, CLASSES * BATCH * PACK], BF16, name="zero_row", align_bytes=64)
         nc.vector.memset(zero_row[:], 0.0)
         first_copy = const.tile([P, 2], BF16, name="first_copy")
@@ -219,6 +239,7 @@ def tile_normalizedlocalmapping_k_kernel(tc, x, weight, bias, out):
             these = jobs[quarter * len(jobs) // OUT_HW : (quarter + 1) * len(jobs) // OUT_HW]
             return [(r, classes, flip(ow, r, classes)) for r, classes in these]
 
+        move_weights(AHEAD)
         pending = flip_batch(1, 0)
         complete = []
         for n in range(len(positions)):
@@ -280,6 +301,8 @@ def tile_normalizedlocalmapping_k_kernel(tc, x, weight, bias, out):
                 )
             if oh % 2 == 1 and ow % 2 == 1:
                 complete.append((oh // 2, ow // 2))
+            if n + 1 + AHEAD < len(positions) - 2:
+                move_weights(n + 1 + AHEAD)
             pending = []
             if oh + 1 < OUT_HW and ow + 1 < OUT_HW:
                 pending = flip_batch(ow + 1, oh + 1)

@@ -22,7 +22,7 @@ OUT_HW = 4
 CLASSES = 4
 PASSES = CLASSES * KER
 HALF = PASSES // 2
-VECTOR_PASSES = 6
+MOVED = 2
 PIXELS = IMG * IMG
 X_CHUNKS = 2
 V_CHUNK = 64 // X_CHUNKS
@@ -75,31 +75,43 @@ def tile_normalizedlocalmapping_k_kernel(tc, x, weight, bias, out):
                         in_=rows[s, e],
                     )
 
-        def regroup_half(n, half):
+        def new_half(n, half):
             grouped[n, half] = grouped_pool.tile(
                 [P, HALF, C_OUT, PACK], BF16, name="half%d" % half, align_bytes=64
             )
-            first = VECTOR_PASSES if half == 0 and n < len(positions) - 1 else 0
-            rows = raw[n][:, half * HALF : (half + 1) * HALF]
-            if first > 0:
-                regroup(nc.vector.tensor_copy, grouped[n, half][:, 0:first], rows[:, 0:first])
-            if half == 0 and n in moved:
-                nc.scalar.copy(
-                    out=grouped[n, half][:, first:HALF].rearrange("p u o t -> p (u o t)"),
-                    in_=moved[n][:].rearrange("p u o t -> p (u o t)"),
-                )
-            else:
-                regroup(nc.scalar.copy, grouped[n, half][:, first:HALF], rows[:, first:HALF])
+
+        def regroup_passes(copy, n, half, first, last):
+            if first < last:
+                rows = raw[n][:, half * HALF + first : half * HALF + last]
+                regroup(copy, grouped[n, half][:, first:last], rows)
+
+        def load_after(n, half):
             if n + RAW_BUFS < len(positions):
                 load_classes(n + RAW_BUFS, (2 * half, 2 * half + 1))
 
+        def regroup_half(n, half):
+            new_half(n, half)
+            by_vector = 0
+            if half == 0 and n < len(positions) - 1:
+                by_vector = 6 if n % 2 == 0 else 4
+            by_scalar = HALF
+            regroup_passes(nc.vector.tensor_copy, n, half, 0, by_vector)
+            if half == 0 and n in moved:
+                by_scalar = HALF - MOVED
+                nc.scalar.copy(
+                    out=grouped[n, half][:, by_scalar:HALF].rearrange("p u o t -> p (u o t)"),
+                    in_=moved[n][:].rearrange("p u o t -> p (u o t)"),
+                )
+            regroup_passes(nc.scalar.copy, n, half, by_vector, by_scalar)
+            load_after(n, half)
+
         def move_weights(n):
-            moved[n] = flip_pool.tile([P, HALF - VECTOR_PASSES, C_OUT, PACK], BF16, name="flipped")
-            for u in range(VECTOR_PASSES, HALF):
+            moved[n] = flip_pool.tile([P, MOVED, C_OUT, PACK], BF16, name="flipped")
+            for u in range(MOVED):
                 nc.tensor.matmul(
-                    moved[n][:, u - VECTOR_PASSES].rearrange("p o t -> p t o"),
+                    moved[n][:, u].rearrange("p o t -> p t o"),
                     lhsT=identity_bf16[:],
-                    rhs=raw[n][:, u],
+                    rhs=raw[n][:, HALF - MOVED + u],
                     start=True,
                     stop=True,
                 )
@@ -128,6 +140,7 @@ def tile_normalizedlocalmapping_k_kernel(tc, x, weight, bias, out):
         nc.scalar.copy(out=first_copy[:], in_=zero_row[:, 0:2])
         zero_words = zero_row[:, 0 : 2 * P].bitcast(F32)
         bias_all = const.tile([P, OUT_HW, OUT_HW, C_OUT], BF16, name="bias_all")
+        partial = const.tile([P, 4, 2, C_OUT], F32, name="partial")
         pooled = const.tile([P, C_OUT, 4], F32, name="pooled")
 
         with tc.tile_pool(name="x_stage", bufs=1) as x_pool:
@@ -139,7 +152,7 @@ def tile_normalizedlocalmapping_k_kernel(tc, x, weight, bias, out):
             def load_image(k):
                 nc.sync.dma_start(out=x_rows[k][:].rearrange("b v s e q -> b (v s e q)"), in_=x_chunks[k])
 
-            load_classes(0, range(CLASSES))
+            load_classes(0, (0, 2, 1, 3))
             load_image(0)
             load_image(1)
             load_classes(1, range(CLASSES))
@@ -160,8 +173,13 @@ def tile_normalizedlocalmapping_k_kernel(tc, x, weight, bias, out):
                         in_=pixels[:, IMG - 1, :, :, 1:IMG].rearrange("b v e (w j) -> b w v e j", j=2),
                     )
 
-            regroup_half(0, 0)
-            regroup_half(0, 1)
+            for half in range(2):
+                new_half(0, half)
+            for first in (0, HALF // 2):
+                regroup_passes(nc.vector.tensor_copy, 0, 0, first, first + HALF // 2)
+                regroup_passes(nc.scalar.copy, 0, 1, first, first + HALF // 2)
+            for half in range(2):
+                load_after(0, half)
             sort_image(0)
             quantise_half(0, 0)
             sort_image(1)
@@ -215,24 +233,17 @@ def tile_normalizedlocalmapping_k_kernel(tc, x, weight, bias, out):
 
         sums = {}
 
-        def pool_window(ph, pw):
-            biased = work.tile([P, 2, 2, C_OUT], F32, name="biased")
+        def add_bias(out, window, a, b):
+            ph, pw = window
             nc.vector.tensor_tensor(
-                out=biased[:],
-                in0=sums[ph, pw][:],
-                in1=bias_all[:, 2 * ph : 2 * ph + 2, 2 * pw : 2 * pw + 2, :],
+                out=out,
+                in0=sums[window][:, a, b, :],
+                in1=bias_all[:, 2 * ph : 2 * ph + 2, 2 * pw : 2 * pw + 2, :][:, a, b, :],
                 op=ADD,
             )
-            row_max = work.tile([P, 2, C_OUT], F32, name="row_max")
-            nc.vector.tensor_tensor(out=row_max[:], in0=biased[:, 0], in1=biased[:, 1], op=MAX)
-            nc.vector.scalar_tensor_tensor(
-                out=pooled[:, :, ph * 2 + pw],
-                in0=row_max[:, 0, :],
-                scalar=0.0,
-                in1=row_max[:, 1, :],
-                op0=MAX,
-                op1=MAX,
-            )
+
+        def larger(out, in0, in1):
+            nc.vector.tensor_tensor(out=out, in0=in0, in1=in1, op=MAX)
 
         def flip_batch(ow, quarter):
             jobs = flip_jobs(ow)
@@ -264,6 +275,25 @@ def tile_normalizedlocalmapping_k_kernel(tc, x, weight, bias, out):
                 groups = [(0, 2), (2, 3), (3, 4)]
             else:
                 groups = [(0, 2), (2, 4)]
+            pooling = []
+            if complete:
+                window = complete.pop()
+                slot = partial[:, window[0] * 2 + window[1]]
+                biased = work.tile([P, 2, 2, C_OUT], F32, name="biased")
+                pooling.append([(add_bias, biased[:], window, slice(0, 2), slice(0, 2))])
+                pooling.append([(larger, slot, biased[:, 0], biased[:, 1])])
+            if n == len(positions) - 1:
+                window = (1, 1)
+                slot = partial[:, 3]
+                biased = work.tile([P, 2, 2, C_OUT], F32, name="biased")
+                pooling.append(
+                    [
+                        (add_bias, biased[:, 0], window, 0, slice(0, 2)),
+                        (add_bias, biased[:, 1, 0], window, 1, 0),
+                    ]
+                )
+                pooling.append([(larger, slot[:, 1], biased[:, 0, 0], biased[:, 0, 1])])
+                pooling.append([(larger, slot[:, 0], slot[:, 1], biased[:, 1, 0])])
             for a, z in groups:
                 r = oh + a - 1
                 if 0 <= r < IMG:
@@ -275,14 +305,14 @@ def tile_normalizedlocalmapping_k_kernel(tc, x, weight, bias, out):
                     scales=p_scales[:, a:z].rearrange("p i s b -> p (i s b)"),
                     in_=image_rows,
                 )
+                for step in pooling[0:1]:
+                    for call in step:
+                        call[0](*call[1:])
+                pooling = pooling[1:]
 
             quantise_half(n, 1)
             if n + AHEAD < len(positions):
                 regroup_half(n + AHEAD, 1)
-
-            for ph, pw in complete:
-                pool_window(ph, pw)
-            complete = []
 
             window = (oh // 2, ow // 2)
             if window not in sums:
@@ -300,7 +330,7 @@ def tile_normalizedlocalmapping_k_kernel(tc, x, weight, bias, out):
                     stop=(u == PASSES - 1),
                 )
             if oh % 2 == 1 and ow % 2 == 1:
-                complete.append((oh // 2, ow // 2))
+                complete.append(window)
             if n + 1 + AHEAD < len(positions) - 2:
                 move_weights(n + 1 + AHEAD)
             pending = []
@@ -311,8 +341,15 @@ def tile_normalizedlocalmapping_k_kernel(tc, x, weight, bias, out):
             if n + 1 < len(positions):
                 quantise_half(n + 1, 0)
 
-        for ph, pw in complete:
-            pool_window(ph, pw)
+        add_bias(partial[:, 3, 1, :], (1, 1), 1, 1)
+        nc.vector.scalar_tensor_tensor(
+            out=pooled[:],
+            in0=partial[:, :, 0, :].rearrange("p w o -> p o w"),
+            scalar=0.0,
+            in1=partial[:, :, 1, :].rearrange("p w o -> p o w"),
+            op0=MAX,
+            op1=MAX,
+        )
         nc.sync.dma_start(
             out=out.rearrange("b o h w -> b (o h w)"),
             in_=pooled[:].rearrange("p o w -> p (o w)"),

@@ -61,19 +61,17 @@ def tile_normalizedlocalmapping_k_kernel(tc, x, weight, bias, out):
         quantised = {}
         moved = {}
 
-        def load_classes(n, classes):
+        def load_half(n, half):
             oh, ow = positions[n]
             rows = weight[oh * OUT_HW + ow].rearrange(
-                "(v s e k) o -> s e v (k o)", s=CLASSES, e=2, k=KER * KER
+                "(v h s e k) o -> h e v s (k o)", h=2, s=CLASSES // 2, e=2, k=KER * KER
             )
-            if n not in raw:
-                raw[n] = raw_pool.tile([P, PASSES, PACK, C_OUT], BF16, name="raw")
-            for s in classes:
-                for e in range(2):
-                    nc.sync.dma_start(
-                        out=raw[n][e:P:2, s * KER : (s + 1) * KER].rearrange("p i t o -> p (i t o)"),
-                        in_=rows[s, e],
-                    )
+            raw[n, half] = raw_pool.tile([P, HALF, PACK, C_OUT], BF16, name="raw%d" % half)
+            for e in range(2):
+                nc.sync.dma_start(
+                    out=raw[n, half][e:P:2].rearrange("p (s i) t o -> p s (i t o)", s=CLASSES // 2),
+                    in_=rows[half, e],
+                )
 
         def new_half(n, half):
             grouped[n, half] = grouped_pool.tile(
@@ -82,12 +80,11 @@ def tile_normalizedlocalmapping_k_kernel(tc, x, weight, bias, out):
 
         def regroup_passes(copy, n, half, first, last):
             if first < last:
-                rows = raw[n][:, half * HALF + first : half * HALF + last]
-                regroup(copy, grouped[n, half][:, first:last], rows)
+                regroup(copy, grouped[n, half][:, first:last], raw[n, half][:, first:last])
 
         def load_after(n, half):
             if n + RAW_BUFS < len(positions):
-                load_classes(n + RAW_BUFS, (2 * half, 2 * half + 1))
+                load_half(n + RAW_BUFS, half)
 
         def regroup_half(n, half):
             new_half(n, half)
@@ -111,7 +108,7 @@ def tile_normalizedlocalmapping_k_kernel(tc, x, weight, bias, out):
                 nc.tensor.matmul(
                     moved[n][:, u].rearrange("p o t -> p t o"),
                     lhsT=identity_bf16[:],
-                    rhs=raw[n][:, HALF - MOVED + u],
+                    rhs=raw[n, 0][:, HALF - MOVED + u],
                     start=True,
                     stop=True,
                 )
@@ -126,9 +123,9 @@ def tile_normalizedlocalmapping_k_kernel(tc, x, weight, bias, out):
             )
             quantised[n, half] = (w_codes, w_scales)
 
-        x_pairs = const.tile([P, CLASSES, IMG, PAIRS, P, 2], BF16, name="x_pairs")
+        x_pairs = const.tile([P, CLASSES, PAIRS, IMG, P, 2], BF16, name="x_pairs")
         nc.gpsimd.memset(
-            x_pairs[:, :, :, 0].rearrange("b s r p j -> b (s r) (p j)").bitcast(U32), 0
+            x_pairs[:, :, 0].rearrange("b s r p j -> b s (r p j)").bitcast(U32), 0
         )
         identity = const.tile([P, P], F32, name="identity")
         masks.make_identity(nc, identity[:])
@@ -152,33 +149,32 @@ def tile_normalizedlocalmapping_k_kernel(tc, x, weight, bias, out):
             def load_image(k):
                 nc.sync.dma_start(out=x_rows[k][:].rearrange("b v s e q -> b (v s e q)"), in_=x_chunks[k])
 
-            load_classes(0, (0, 2, 1, 3))
-            load_image(0)
-            load_image(1)
-            load_classes(1, range(CLASSES))
-            load_classes(2, range(CLASSES))
+            for half in (1, 0):
+                load_half(0, half)
+            for k in range(X_CHUNKS):
+                load_image(k)
+            for n in range(1, RAW_BUFS):
+                for half in range(2):
+                    load_half(n, half)
 
             def sort_image(k):
                 for s in range(CLASSES):
                     mine = slice(2 * V_CHUNK * k, 2 * V_CHUNK * (k + 1))
-                    pairs = x_pairs[:, s, :, :, mine].rearrange("b r w (v e) j -> b r w v e j", e=2)
+                    pairs = x_pairs[:, s, :, :, mine].rearrange("b w r (v e) j -> b w r v e j", e=2)
                     pixels = x_rows[k][:, :, s].rearrange("b v e (r c) -> b r v e c", c=IMG)
-                    nc.scalar.copy(out=pairs[:, :, 0, :, :, 1], in_=pixels[:, :, :, :, 0])
+                    nc.scalar.copy(out=pairs[:, 0, :, :, :, 1], in_=pixels[:, :, :, :, 0])
                     for w in range(1, PAIRS):
                         nc.vector.tensor_copy(
-                            out=pairs[:, 0 : IMG - 1, w], in_=pixels[:, 0 : IMG - 1, :, :, 2 * w - 1 : 2 * w + 1]
+                            out=pairs[:, w, 0 : IMG - 1], in_=pixels[:, 0 : IMG - 1, :, :, 2 * w - 1 : 2 * w + 1]
                         )
                     nc.vector.tensor_copy(
-                        out=pairs[:, IMG - 1, 1:PAIRS],
+                        out=pairs[:, 1:PAIRS, IMG - 1],
                         in_=pixels[:, IMG - 1, :, :, 1:IMG].rearrange("b v e (w j) -> b w v e j", j=2),
                     )
 
             for half in range(2):
                 new_half(0, half)
-            for first in (0, HALF // 2):
-                regroup_passes(nc.vector.tensor_copy, 0, 0, first, first + HALF // 2)
-                regroup_passes(nc.scalar.copy, 0, 1, first, first + HALF // 2)
-            for half in range(2):
+                regroup_passes(nc.vector.tensor_copy if half == 0 else nc.scalar.copy, 0, half, 0, HALF)
                 load_after(0, half)
             sort_image(0)
             quantise_half(0, 0)
@@ -199,7 +195,7 @@ def tile_normalizedlocalmapping_k_kernel(tc, x, weight, bias, out):
             for a in range(len(classes)):
                 for h in range(len(pairs)):
                     if pairs[h] < PAIRS:
-                        words = x_pairs[:, classes[a], r, pairs[h]].rearrange("b p j -> b (p j)").bitcast(F32)
+                        words = x_pairs[:, classes[a], pairs[h], r].rearrange("b p j -> b (p j)").bitcast(F32)
                     else:
                         words = zero_words
                     target = flipped[:, a, h, :] if ow % 2 == 0 else flipped[:, a, :, h]

@@ -22,6 +22,7 @@ OUT_HW = 4
 CLASSES = 4
 PASSES = CLASSES * KER
 HALF = PASSES // 2
+VECTOR_PASSES = 6
 MOVED = 2
 PIXELS = IMG * IMG
 X_CHUNKS = 2
@@ -88,9 +89,7 @@ def tile_normalizedlocalmapping_k_kernel(tc, x, weight, bias, out):
 
         def regroup_half(n, half):
             new_half(n, half)
-            by_vector = 0
-            if half == 0 and n < len(positions) - 1:
-                by_vector = 6 if n % 2 == 0 else 4
+            by_vector = VECTOR_PASSES if half == 0 else 0
             by_scalar = HALF
             regroup_passes(nc.vector.tensor_copy, n, half, 0, by_vector)
             if half == 0 and n in moved:
@@ -123,10 +122,9 @@ def tile_normalizedlocalmapping_k_kernel(tc, x, weight, bias, out):
             )
             quantised[n, half] = (w_codes, w_scales)
 
-        x_pairs = const.tile([P, CLASSES, PAIRS, IMG, P, 2], BF16, name="x_pairs")
-        nc.gpsimd.memset(
-            x_pairs[:, :, 0].rearrange("b s r p j -> b s (r p j)").bitcast(U32), 0
-        )
+        inner = const.tile([P, CLASSES, IMG, P, IMG - 1], BF16, name="inner")
+        edge = const.tile([P, CLASSES, IMG, P, 2], BF16, name="edge")
+        nc.gpsimd.memset(edge[:].rearrange("b s r p c -> b (s r p c)").bitcast(U32), 0)
         identity = const.tile([P, P], F32, name="identity")
         masks.make_identity(nc, identity[:])
         identity_bf16 = const.tile([P, P], BF16, name="identity_bf16")
@@ -158,19 +156,20 @@ def tile_normalizedlocalmapping_k_kernel(tc, x, weight, bias, out):
                     load_half(n, half)
 
             def sort_image(k):
+                mine = slice(2 * V_CHUNK * k, 2 * V_CHUNK * (k + 1))
                 for s in range(CLASSES):
-                    mine = slice(2 * V_CHUNK * k, 2 * V_CHUNK * (k + 1))
-                    pairs = x_pairs[:, s, :, :, mine].rearrange("b w r (v e) j -> b w r v e j", e=2)
                     pixels = x_rows[k][:, :, s].rearrange("b v e (r c) -> b r v e c", c=IMG)
-                    nc.scalar.copy(out=pairs[:, 0, :, :, :, 1], in_=pixels[:, :, :, :, 0])
-                    for w in range(1, PAIRS):
-                        nc.vector.tensor_copy(
-                            out=pairs[:, w, 0 : IMG - 1], in_=pixels[:, 0 : IMG - 1, :, :, 2 * w - 1 : 2 * w + 1]
-                        )
-                    nc.vector.tensor_copy(
-                        out=pairs[:, 1:PAIRS, IMG - 1],
-                        in_=pixels[:, IMG - 1, :, :, 1:IMG].rearrange("b v e (w j) -> b w v e j", j=2),
+                    nc.scalar.copy(
+                        out=edge[:, s, :, mine, 1].rearrange("b r (v e) -> b r v e", e=2), in_=pixels[:, :, :, :, 0]
                     )
+                    nc.vector.tensor_copy(
+                        out=inner[:, s, 0 : IMG - 1, mine, :].rearrange("b r (v e) c -> b r v e c", e=2),
+                        in_=pixels[:, 0 : IMG - 1, :, :, 1:IMG],
+                    )
+                nc.vector.tensor_copy(
+                    out=inner[:, :, IMG - 1, mine, :].rearrange("b s (v e) c -> b s v e c", e=2),
+                    in_=x_rows[k][:, :, :, :, PIXELS - IMG + 1 : PIXELS].rearrange("b v s e c -> b s v e c"),
+                )
 
             for half in range(2):
                 new_half(0, half)
@@ -194,8 +193,11 @@ def tile_normalizedlocalmapping_k_kernel(tc, x, weight, bias, out):
                 flipped = flip_pool.tile([P, len(classes), BATCH, len(pairs)], F32, name="flipped")
             for a in range(len(classes)):
                 for h in range(len(pairs)):
-                    if pairs[h] < PAIRS:
-                        words = x_pairs[:, classes[a], pairs[h], r].rearrange("b p j -> b (p j)").bitcast(F32)
+                    if pairs[h] == 0:
+                        words = edge[:, classes[a], r].rearrange("b p c -> b (p c)").bitcast(F32)
+                    elif pairs[h] < PAIRS:
+                        words = inner[:, classes[a], r].rearrange("b p c -> b (p c)").bitcast(F32)
+                        words = words[:, pairs[h] - 1 : 2 * P : 2]
                     else:
                         words = zero_words
                     target = flipped[:, a, h, :] if ow % 2 == 0 else flipped[:, a, :, h]

@@ -17,6 +17,7 @@ RUN = 4
 BATCH = 128
 C_OUT = 128
 IMG = 5
+PADDED = IMG + 2
 KER = 4
 OUT_HW = 4
 CLASSES = 4
@@ -52,10 +53,9 @@ def tile_normalizedlocalmapping_k_kernel(tc, x, weight, bias, out):
         grouped_pool = ctx.enter_context(tc.tile_pool(name="grouped", bufs=2))
         w_pool = ctx.enter_context(tc.tile_pool(name="w_codes", bufs=2))
         p_pool = ctx.enter_context(tc.tile_pool(name="p_codes", bufs=2))
-        window_pool = ctx.enter_context(tc.tile_pool(name="windows", bufs=2))
         work = ctx.enter_context(tc.tile_pool(name="work", bufs=1))
-        acc_pool = ctx.enter_context(tc.psum_pool(name="acc", bufs=3))
-        flip_pool = ctx.enter_context(tc.psum_pool(name="flip", bufs=5))
+        acc_pool = ctx.enter_context(tc.psum_pool(name="acc", bufs=2))
+        flip_pool = ctx.enter_context(tc.psum_pool(name="flip", bufs=6))
 
         raw = {}
         grouped = {}
@@ -87,19 +87,26 @@ def tile_normalizedlocalmapping_k_kernel(tc, x, weight, bias, out):
             if n + RAW_BUFS < len(positions):
                 load_half(n + RAW_BUFS, half)
 
-        def regroup_half(n, half):
+
+        def vector_regroups(n):
+            regroup_passes(nc.vector.tensor_copy, n, 0, 0, VECTOR_PASSES)
+            load_after(n, 0)
+
+        def scalar_regroups(n, half):
             new_half(n, half)
-            by_vector = VECTOR_PASSES if half == 0 else 0
-            by_scalar = HALF
-            regroup_passes(nc.vector.tensor_copy, n, half, 0, by_vector)
+            first = VECTOR_PASSES if half == 0 else 0
+            last = HALF
             if half == 0 and n in moved:
-                by_scalar = HALF - MOVED
+                last = HALF - MOVED
                 nc.scalar.copy(
-                    out=grouped[n, half][:, by_scalar:HALF].rearrange("p u o t -> p (u o t)"),
+                    out=grouped[n, half][:, last:HALF].rearrange("p u o t -> p (u o t)"),
                     in_=moved[n][:].rearrange("p u o t -> p (u o t)"),
                 )
-            regroup_passes(nc.scalar.copy, n, half, by_vector, by_scalar)
-            load_after(n, half)
+            middle = (first + last) // 2 if half == 1 and n == len(positions) - 1 else last
+            regroup_passes(nc.scalar.copy, n, half, first, middle)
+            regroup_passes(nc.scalar.copy, n, half, middle, last)
+            if half == 1:
+                load_after(n, half)
 
         def move_weights(n):
             moved[n] = flip_pool.tile([P, MOVED, C_OUT, PACK], BF16, name="flipped")
@@ -115,11 +122,14 @@ def tile_normalizedlocalmapping_k_kernel(tc, x, weight, bias, out):
         def quantise_half(n, half):
             w_codes = w_pool.tile([P, HALF, C_OUT], U32, name="w_codes%d" % half, align_bytes=64)
             w_scales = w_pool.tile([P, HALF, C_OUT], U8, name="w_scales%d" % half, align_bytes=64)
-            nc.vector.quantize_mx(
-                out=w_codes[:].rearrange("p u o -> p (u o)").bitcast(FP8X4),
-                scales=w_scales[:].rearrange("p u o -> p (u o)"),
-                in_=grouped[n, half][:].rearrange("p u o t -> p (u o t)"),
-            )
+            size = HALF // 2 if half == 1 and n == len(positions) - 1 else HALF
+            for first in range(0, HALF, size):
+                these = slice(first, first + size)
+                nc.vector.quantize_mx(
+                    out=w_codes[:, these].rearrange("p u o -> p (u o)").bitcast(FP8X4),
+                    scales=w_scales[:, these].rearrange("p u o -> p (u o)"),
+                    in_=grouped[n, half][:, these].rearrange("p u o t -> p (u o t)"),
+                )
             quantised[n, half] = (w_codes, w_scales)
 
         inner = const.tile([P, CLASSES, IMG, P, IMG - 1], BF16, name="inner")
@@ -129,12 +139,24 @@ def tile_normalizedlocalmapping_k_kernel(tc, x, weight, bias, out):
         masks.make_identity(nc, identity[:])
         identity_bf16 = const.tile([P, P], BF16, name="identity_bf16")
         masks.make_identity(nc, identity_bf16[:])
-        zero_row = const.tile([P, CLASSES * BATCH * PACK], BF16, name="zero_row", align_bytes=64)
-        nc.vector.memset(zero_row[:], 0.0)
+        zeros = const.tile([P, 2 * P], BF16, name="zeros")
+        nc.vector.memset(zeros[:], 0.0)
         first_copy = const.tile([P, 2], BF16, name="first_copy")
-        nc.scalar.copy(out=first_copy[:], in_=zero_row[:, 0:2])
-        zero_words = zero_row[:, 0 : 2 * P].bitcast(F32)
+        nc.scalar.copy(out=first_copy[:], in_=zeros[:, 0:2])
+        zero_words = zeros[:].bitcast(F32)
         bias_all = const.tile([P, OUT_HW, OUT_HW, C_OUT], BF16, name="bias_all")
+        windows = []
+
+        def new_windows(pool, memset):
+            windows.append(
+                pool.tile(
+                    [P, PADDED, CLASSES, BATCH, PACK], BF16, name="windows%d" % len(windows), align_bytes=64
+                )
+            )
+            for i in (0, PADDED - 1):
+                memset(windows[-1][:, i].rearrange("p s b t -> p (s b t)").bitcast(U32), 0)
+
+        new_windows(const, nc.gpsimd.memset)
         partial = const.tile([P, 4, 2, C_OUT], F32, name="partial")
         pooled = const.tile([P, C_OUT, 4], F32, name="pooled")
 
@@ -171,15 +193,13 @@ def tile_normalizedlocalmapping_k_kernel(tc, x, weight, bias, out):
                     in_=x_rows[k][:, :, :, :, PIXELS - IMG + 1 : PIXELS].rearrange("b v s e c -> b s v e c"),
                 )
 
-            for half in range(2):
-                new_half(0, half)
-                regroup_passes(nc.vector.tensor_copy if half == 0 else nc.scalar.copy, 0, half, 0, HALF)
-                load_after(0, half)
+            for half in (1, 0):
+                scalar_regroups(0, half)
+            vector_regroups(0)
+            quantise_half(0, 1)
             sort_image(0)
             quantise_half(0, 0)
             sort_image(1)
-
-        windows = {}
 
         def flip_jobs(ow):
             step = 2 if ow % 2 == 0 else 1
@@ -205,7 +225,7 @@ def tile_normalizedlocalmapping_k_kernel(tc, x, weight, bias, out):
             return flipped
 
         def unload(copy, ow, r, classes, flipped):
-            target = windows[ow][:, r, classes[0] : classes[-1] + 1]
+            target = windows[ow % 2][:, r + 1, classes[0] : classes[-1] + 1]
             if ow % 2 == 0:
                 copy(
                     out=target.rearrange("p s b t -> p (s b t)")
@@ -220,14 +240,12 @@ def tile_normalizedlocalmapping_k_kernel(tc, x, weight, bias, out):
                     in_=columns.rearrange("p (b k) -> p b k", k=6)[:, :, 1:5],
                 )
 
-        def new_windows(ow):
-            windows[ow] = window_pool.tile([P, IMG, CLASSES, BATCH, PACK], BF16, name="windows", align_bytes=64)
-
-        regroup_half(1, 0)
-        new_windows(0)
+        scalar_regroups(1, 0)
+        vector_regroups(1)
+        new_windows(ctx.enter_context(tc.tile_pool(name="late", bufs=1)), nc.vector.memset)
         for r, classes in flip_jobs(0):
-            unload(nc.scalar.copy if classes[0] == 0 else nc.vector.tensor_copy, 0, r, classes, flip(0, r, classes))
-        regroup_half(1, 1)
+            unload(nc.scalar.copy, 0, r, classes, flip(0, r, classes))
+        scalar_regroups(1, 1)
 
         sums = {}
 
@@ -254,25 +272,17 @@ def tile_normalizedlocalmapping_k_kernel(tc, x, weight, bias, out):
         for n in range(len(positions)):
             oh, ow = positions[n]
             if n + AHEAD < len(positions):
-                regroup_half(n + AHEAD, 0)
+                scalar_regroups(n + AHEAD, 0)
             if n == 1:
                 nc.sync.dma_start(
                     out=bias_all[:].rearrange("p a b o -> p (a b o)"),
                     in_=bias.rearrange("l o -> (l o)").partition_broadcast(P),
                 )
-            if oh == 0 and ow + 1 < OUT_HW:
-                new_windows(ow + 1)
             for r, classes, flipped in pending:
                 unload(nc.scalar.copy, ow + 1, r, classes, flipped)
 
             p_codes = p_pool.tile([P, KER, CLASSES, BATCH], U32, name="p_codes", align_bytes=64)
             p_scales = p_pool.tile([P, KER, CLASSES, BATCH], U8, name="p_scales", align_bytes=64)
-            if oh == 0:
-                groups = [(0, 1), (1, 3), (3, 4)]
-            elif oh == OUT_HW - 1:
-                groups = [(0, 2), (2, 3), (3, 4)]
-            else:
-                groups = [(0, 2), (2, 4)]
             pooling = []
             if complete:
                 window = complete.pop()
@@ -292,38 +302,39 @@ def tile_normalizedlocalmapping_k_kernel(tc, x, weight, bias, out):
                 )
                 pooling.append([(larger, slot[:, 1], biased[:, 0, 0], biased[:, 0, 1])])
                 pooling.append([(larger, slot[:, 0], slot[:, 1], biased[:, 1, 0])])
-            for a, z in groups:
-                r = oh + a - 1
-                if 0 <= r < IMG:
-                    image_rows = windows[ow][:, r : r + z - a].rearrange("p i s b t -> p (i s b t)")
-                else:
-                    image_rows = zero_row[:]
+            for i in range(0, KER, 2):
                 nc.vector.quantize_mx(
-                    out=p_codes[:, a:z].rearrange("p i s b -> p (i s b)").bitcast(FP8X4),
-                    scales=p_scales[:, a:z].rearrange("p i s b -> p (i s b)"),
-                    in_=image_rows,
+                    out=p_codes[:, i : i + 2].rearrange("p i s b -> p (i s b)").bitcast(FP8X4),
+                    scales=p_scales[:, i : i + 2].rearrange("p i s b -> p (i s b)"),
+                    in_=windows[ow % 2][:, oh + i : oh + i + 2].rearrange("p i s b t -> p (i s b t)"),
                 )
                 for step in pooling[0:1]:
                     for call in step:
                         call[0](*call[1:])
                 pooling = pooling[1:]
 
-            quantise_half(n, 1)
             if n + AHEAD < len(positions):
-                regroup_half(n + AHEAD, 1)
+                vector_regroups(n + AHEAD)
+            if n > 0:
+                quantise_half(n, 1)
+            for step in pooling:
+                for call in step:
+                    call[0](*call[1:])
+            if n + AHEAD < len(positions):
+                scalar_regroups(n + AHEAD, 1)
 
             window = (oh // 2, ow // 2)
             if window not in sums:
                 sums[window] = acc_pool.tile([P, 2, 2, C_OUT], F32, name="sums")
             for u in range(PASSES):
-                half, i, s = u // HALF, u % HALF // 2, u // HALF * 2 + u % 2
-                w_codes, w_scales = quantised[n, half]
+                s, i = u // KER, u % KER
+                w_codes, w_scales = quantised[n, u // HALF]
                 nc.tensor.matmul_mx(
                     out=sums[window][:, oh % 2, ow % 2, :],
                     lhsT=p_codes[:, i, s, :].bitcast(FP8X4),
                     lhsT_scale=p_scales[:, i, s, :],
-                    rhs=w_codes[:, s % 2 * KER + i, :].bitcast(FP8X4),
-                    rhs_scale=w_scales[:, s % 2 * KER + i, :],
+                    rhs=w_codes[:, u % HALF, :].bitcast(FP8X4),
+                    rhs_scale=w_scales[:, u % HALF, :],
                     start=(u == 0),
                     stop=(u == PASSES - 1),
                 )

from contextlib import ExitStack

import concourse.masks as masks
import concourse.mybir as mybir

BF16 = mybir.dt.bfloat16
F32 = mybir.dt.float32
U32 = mybir.dt.uint32
U8 = mybir.dt.uint8
FP8X4 = mybir.dt.float8_e4m3fn_x4
MAX = mybir.AluOpType.max
ADD = mybir.AluOpType.add

P = 128
PACK = 4
RUN = 4
BATCH = 128
C_OUT = 128
IMG = 5
PADDED = IMG + 2
KER = 4
OUT_HW = 4
CLASSES = 4
PASSES = CLASSES * KER
HALF = PASSES // 2
VECTOR_PASSES = 6
MOVED = 2
PIXELS = IMG * IMG
X_CHUNKS = 2
V_CHUNK = 64 // X_CHUNKS
PAIRS = 3
RAW_BUFS = 3
AHEAD = 2

FLOPS = 2 * BATCH * (512 * KER * KER) * C_OUT * OUT_HW * OUT_HW


def regroup(copy, grouped, rows):
    copy(
        out=grouped.rearrange("p u (c n) t -> p u c t n", n=RUN),
        in_=rows.rearrange("p u t (c n) -> p u c t n", n=RUN),
    )


def tile_normalizedlocalmapping_k_kernel(tc, x, weight, bias, out):
    nc = tc.nc
    positions = [(oh, ow) for ow in range(OUT_HW) for oh in range(OUT_HW)]

    with ExitStack() as ctx:
        ctx.enter_context(tc.manual_schedule())
        const = ctx.enter_context(tc.tile_pool(name="const", bufs=1))
        raw_pool = ctx.enter_context(tc.tile_pool(name="raw", bufs=RAW_BUFS))
        grouped_pool = ctx.enter_context(tc.tile_pool(name="grouped", bufs=2))
        w_pool = ctx.enter_context(tc.tile_pool(name="w_codes", bufs=2))
        p_pool = ctx.enter_context(tc.tile_pool(name="p_codes", bufs=2))
        work = ctx.enter_context(tc.tile_pool(name="work", bufs=1))
        acc_pool = ctx.enter_context(tc.psum_pool(name="acc", bufs=2))
        flip_pool = ctx.enter_context(tc.psum_pool(name="flip", bufs=6))

        raw = {}
        grouped = {}
        quantised = {}
        moved = {}

        def load_half(n, half):
            oh, ow = positions[n]
            rows = weight[oh * OUT_HW + ow].rearrange(
                "(v h s e k) o -> h e v s (k o)", h=2, s=CLASSES // 2, e=2, k=KER * KER
            )
            raw[n, half] = raw_pool.tile([P, HALF, PACK, C_OUT], BF16, name="raw%d" % half)
            for e in range(2):
                nc.sync.dma_start(
                    out=raw[n, half][e:P:2].rearrange("p (s i) t o -> p s (i t o)", s=CLASSES // 2),
                    in_=rows[half, e],
                )

        def new_half(n, half):
            grouped[n, half] = grouped_pool.tile(
                [P, HALF, C_OUT, PACK], BF16, name="half%d" % half, align_bytes=64
            )

        def regroup_passes(copy, n, half, first, last):
            if first < last:
                regroup(copy, grouped[n, half][:, first:last], raw[n, half][:, first:last])

        def load_after(n, half):
            if n + RAW_BUFS < len(positions):
                load_half(n + RAW_BUFS, half)


        def vector_regroups(n):
            regroup_passes(nc.vector.tensor_copy, n, 0, 0, VECTOR_PASSES)
            load_after(n, 0)

        def scalar_regroups(n, half):
            new_half(n, half)
            first = VECTOR_PASSES if half == 0 else 0
            last = HALF
            if half == 0 and n in moved:
                last = HALF - MOVED
                nc.scalar.copy(
                    out=grouped[n, half][:, last:HALF].rearrange("p u o t -> p (u o t)"),
                    in_=moved[n][:].rearrange("p u o t -> p (u o t)"),
                )
            middle = (first + last) // 2 if half == 1 and n == len(positions) - 1 else last
            regroup_passes(nc.scalar.copy, n, half, first, middle)
            regroup_passes(nc.scalar.copy, n, half, middle, last)
            if half == 1:
                load_after(n, half)

        def move_weights(n):
            moved[n] = flip_pool.tile([P, MOVED, C_OUT, PACK], BF16, name="flipped")
            for u in range(MOVED):
                nc.tensor.matmul(
                    moved[n][:, u].rearrange("p o t -> p t o"),
                    lhsT=identity_bf16[:],
                    rhs=raw[n, 0][:, HALF - MOVED + u],
                    start=True,
                    stop=True,
                )

        def quantise_half(n, half):
            w_codes = w_pool.tile([P, HALF, C_OUT], U32, name="w_codes%d" % half, align_bytes=64)
            w_scales = w_pool.tile([P, HALF, C_OUT], U8, name="w_scales%d" % half, align_bytes=64)
            size = HALF // 2 if half == 1 and n == len(positions) - 1 else HALF
            for first in range(0, HALF, size):
                these = slice(first, first + size)
                nc.vector.quantize_mx(
                    out=w_codes[:, these].rearrange("p u o -> p (u o)").bitcast(FP8X4),
                    scales=w_scales[:, these].rearrange("p u o -> p (u o)"),
                    in_=grouped[n, half][:, these].rearrange("p u o t -> p (u o t)"),
                )
            quantised[n, half] = (w_codes, w_scales)

        inner = const.tile([P, CLASSES, IMG, P, IMG - 1], BF16, name="inner")
        edge = const.tile([P, CLASSES, IMG, P, 2], BF16, name="edge")
        nc.gpsimd.memset(edge[:].rearrange("b s r p c -> b (s r p c)").bitcast(U32), 0)
        identity = const.tile([P, P], F32, name="identity")
        masks.make_identity(nc, identity[:])
        identity_bf16 = const.tile([P, P], BF16, name="identity_bf16")
        masks.make_identity(nc, identity_bf16[:])
        zeros = const.tile([P, 2 * P], BF16, name="zeros")
        nc.vector.memset(zeros[:], 0.0)
        first_copy = const.tile([P, 2], BF16, name="first_copy")
        nc.scalar.copy(out=first_copy[:], in_=zeros[:, 0:2])
        zero_words = zeros[:].bitcast(F32)
        bias_all = const.tile([P, OUT_HW, OUT_HW, C_OUT], BF16, name="bias_all")
        windows = []

        def new_windows(pool, memset):
            windows.append(
                pool.tile(
                    [P, PADDED, CLASSES, BATCH, PACK], BF16, name="windows%d" % len(windows), align_bytes=64
                )
            )
            for i in (0, PADDED - 1):
                memset(windows[-1][:, i].rearrange("p s b t -> p (s b t)").bitcast(U32), 0)

        new_windows(const, nc.gpsimd.memset)
        partial = const.tile([P, 4, 2, C_OUT], F32, name="partial")
        pooled = const.tile([P, C_OUT, 4], F32, name="pooled")

        with tc.tile_pool(name="x_stage", bufs=1) as x_pool:
            x_chunks = x.rearrange("b (k c) h w -> k b (c h w)", k=X_CHUNKS)
            x_rows = []
            for k in range(X_CHUNKS):
                x_rows.append(x_pool.tile([P, V_CHUNK, CLASSES, 2, PIXELS], BF16, name="x_rows%d" % k))

            def load_image(k):
                nc.sync.dma_start(out=x_rows[k][:].rearrange("b v s e q -> b (v s e q)"), in_=x_chunks[k])

            for half in (1, 0):
                load_half(0, half)
            for k in range(X_CHUNKS):
                load_image(k)
            for n in range(1, RAW_BUFS):
                for half in range(2):
                    load_half(n, half)

            def sort_image(k):
                mine = slice(2 * V_CHUNK * k, 2 * V_CHUNK * (k + 1))
                for s in range(CLASSES):
                    pixels = x_rows[k][:, :, s].rearrange("b v e (r c) -> b r v e c", c=IMG)
                    nc.scalar.copy(
                        out=edge[:, s, :, mine, 1].rearrange("b r (v e) -> b r v e", e=2), in_=pixels[:, :, :, :, 0]
                    )
                    nc.vector.tensor_copy(
                        out=inner[:, s, 0 : IMG - 1, mine, :].rearrange("b r (v e) c -> b r v e c", e=2),
                        in_=pixels[:, 0 : IMG - 1, :, :, 1:IMG],
                    )
                nc.vector.tensor_copy(
                    out=inner[:, :, IMG - 1, mine, :].rearrange("b s (v e) c -> b s v e c", e=2),
                    in_=x_rows[k][:, :, :, :, PIXELS - IMG + 1 : PIXELS].rearrange("b v s e c -> b s v e c"),
                )

            for half in (1, 0):
                scalar_regroups(0, half)
            vector_regroups(0)
            quantise_half(0, 1)
            sort_image(0)
            quantise_half(0, 0)
            sort_image(1)

        def flip_jobs(ow):
            step = 2 if ow % 2 == 0 else 1
            return [(r, list(range(s, s + step))) for r in range(IMG) for s in range(0, CLASSES, step)]

        def flip(ow, r, classes):
            pairs = list(range(ow // 2, ow // 2 + (2 if ow % 2 == 0 else 3)))
            if ow % 2 == 0:
                flipped = flip_pool.tile([P, len(classes), len(pairs), BATCH], F32, name="flipped")
            else:
                flipped = flip_pool.tile([P, len(classes), BATCH, len(pairs)], F32, name="flipped")
            for a in range(len(classes)):
                for h in range(len(pairs)):
                    if pairs[h] == 0:
                        words = edge[:, classes[a], r].rearrange("b p c -> b (p c)").bitcast(F32)
                    elif pairs[h] < PAIRS:
                        words = inner[:, classes[a], r].rearrange("b p c -> b (p c)").bitcast(F32)
                        words = words[:, pairs[h] - 1 : 2 * P : 2]
                    else:
                        words = zero_words
                    target = flipped[:, a, h, :] if ow % 2 == 0 else flipped[:, a, :, h]
                    nc.tensor.transpose(target, words, identity[:])
            return flipped

        def unload(copy, ow, r, classes, flipped):
            target = windows[ow % 2][:, r + 1, classes[0] : classes[-1] + 1]
            if ow % 2 == 0:
                copy(
                    out=target.rearrange("p s b t -> p (s b t)")
                    .bitcast(F32)
                    .rearrange("p (s b h) -> p s b h", s=2, h=2),
                    in_=flipped[:].rearrange("p s h b -> p s b h"),
                )
            else:
                columns = flipped[:].rearrange("p s b h -> p (s b h)").bitcast(BF16)
                copy(
                    out=target.rearrange("p s b t -> p (s b) t"),
                    in_=columns.rearrange("p (b k) -> p b k", k=6)[:, :, 1:5],
                )

        scalar_regroups(1, 0)
        vector_regroups(1)
        new_windows(ctx.enter_context(tc.tile_pool(name="late", bufs=1)), nc.vector.memset)
        for r, classes in flip_jobs(0):
            unload(nc.scalar.copy, 0, r, classes, flip(0, r, classes))
        scalar_regroups(1, 1)

        sums = {}

        def add_bias(out, window, a, b):
            ph, pw = window
            nc.vector.tensor_tensor(
                out=out,
                in0=sums[window][:, a, b, :],
                in1=bias_all[:, 2 * ph : 2 * ph + 2, 2 * pw : 2 * pw + 2, :][:, a, b, :],
                op=ADD,
            )

        def larger(out, in0, in1):
            nc.vector.tensor_tensor(out=out, in0=in0, in1=in1, op=MAX)

        def flip_batch(ow, quarter):
            jobs = flip_jobs(ow)
            these = jobs[quarter * len(jobs) // OUT_HW : (quarter + 1) * len(jobs) // OUT_HW]
            return [(r, classes, flip(ow, r, classes)) for r, classes in these]

        move_weights(AHEAD)
        pending = flip_batch(1, 0)
        complete = []
        for n in range(len(positions)):
            oh, ow = positions[n]
            if n + AHEAD < len(positions):
                scalar_regroups(n + AHEAD, 0)
            if n == 1:
                nc.sync.dma_start(
                    out=bias_all[:].rearrange("p a b o -> p (a b o)"),
                    in_=bias.rearrange("l o -> (l o)").partition_broadcast(P),
                )
            for r, classes, flipped in pending:
                unload(nc.scalar.copy, ow + 1, r, classes, flipped)

            p_codes = p_pool.tile([P, KER, CLASSES, BATCH], U32, name="p_codes", align_bytes=64)
            p_scales = p_pool.tile([P, KER, CLASSES, BATCH], U8, name="p_scales", align_bytes=64)
            pooling = []
            if complete:
                window = complete.pop()
                slot = partial[:, window[0] * 2 + window[1]]
                biased = work.tile([P, 2, 2, C_OUT], F32, name="biased")
                pooling.append([(add_bias, biased[:], window, slice(0, 2), slice(0, 2))])
                pooling.append([(larger, slot, biased[:, 0], biased[:, 1])])
            if n == len(positions) - 1:
                window = (1, 1)
                slot = partial[:, 3]
                biased = work.tile([P, 2, 2, C_OUT], F32, name="biased")
                pooling.append(
                    [
                        (add_bias, biased[:, 0], window, 0, slice(0, 2)),
                        (add_bias, biased[:, 1, 0], window, 1, 0),
                    ]
                )
                pooling.append([(larger, slot[:, 1], biased[:, 0, 0], biased[:, 0, 1])])
                pooling.append([(larger, slot[:, 0], slot[:, 1], biased[:, 1, 0])])
            for i in range(0, KER, 2):
                nc.vector.quantize_mx(
                    out=p_codes[:, i : i + 2].rearrange("p i s b -> p (i s b)").bitcast(FP8X4),
                    scales=p_scales[:, i : i + 2].rearrange("p i s b -> p (i s b)"),
                    in_=windows[ow % 2][:, oh + i : oh + i + 2].rearrange("p i s b t -> p (i s b t)"),
                )
                for step in pooling[0:1]:
                    for call in step:
                        call[0](*call[1:])
                pooling = pooling[1:]

            if n + AHEAD < len(positions):
                vector_regroups(n + AHEAD)
            if n > 0:
                quantise_half(n, 1)
            for step in pooling:
                for call in step:
                    call[0](*call[1:])
            if n + AHEAD < len(positions):
                scalar_regroups(n + AHEAD, 1)

            window = (oh // 2, ow // 2)
            if window not in sums:
                sums[window] = acc_pool.tile([P, 2, 2, C_OUT], F32, name="sums")
            for u in range(PASSES):
                s, i = u // KER, u % KER
                w_codes, w_scales = quantised[n, u // HALF]
                nc.tensor.matmul_mx(
                    out=sums[window][:, oh % 2, ow % 2, :],
                    lhsT=p_codes[:, i, s, :].bitcast(FP8X4),
                    lhsT_scale=p_scales[:, i, s, :],
                    rhs=w_codes[:, u % HALF, :].bitcast(FP8X4),
                    rhs_scale=w_scales[:, u % HALF, :],
                    start=(u == 0),
                    stop=(u == PASSES - 1),
                )
            if oh % 2 == 1 and ow % 2 == 1:
                complete.append(window)
            if n + 1 + AHEAD < len(positions) - 2:
                move_weights(n + 1 + AHEAD)
            pending = []
            if oh + 1 < OUT_HW and ow + 1 < OUT_HW:
                pending = flip_batch(ow + 1, oh + 1)
            elif ow + 2 < OUT_HW:
                pending = flip_batch(ow + 2, 0)
            if n + 1 < len(positions):
                quantise_half(n + 1, 0)

        add_bias(partial[:, 3, 1, :], (1, 1), 1, 1)
        nc.vector.scalar_tensor_tensor(
            out=pooled[:],
            in0=partial[:, :, 0, :].rearrange("p w o -> p o w"),
            scalar=0.0,
            in1=partial[:, :, 1, :].rearrange("p w o -> p o w"),
            op0=MAX,
            op1=MAX,
        )
        nc.sync.dma_start(
            out=out.rearrange("b o h w -> b (o h w)"),
            in_=pooled[:].rearrange("p o w -> p (o w)"),
        )
